import numpy as np
import ml_dtypes


def mxq(x, axis, fmt="e4m3"):
    dtype, down = {"e4m3": (ml_dtypes.float8_e4m3fn, 7), "e5m2": (ml_dtypes.float8_e5m2, 14)}[fmt]
    v = np.moveaxis(np.asarray(x, np.float32).astype(ml_dtypes.bfloat16).astype(np.float64), axis, -1)
    blocks = v.reshape(v.shape[:-1] + (-1, 32))
    amax = np.abs(blocks).max(-1, keepdims=True)
    byte = np.maximum(np.where(amax > 0, np.frexp(amax)[1] - 1 + 127, 0) - down, 1)
    scale = np.exp2(byte - 127.0)
    codes = (blocks / scale).astype(np.float32).astype(dtype).astype(np.float64)
    return np.moveaxis((codes * scale).reshape(v.shape), -1, axis)


WIDE = False


def mx_kscale(k):
    if not WIDE:
        return np.ones(k)
    levels = np.array([18, -18])
    if k % 512:
        return np.exp2(np.random.permutation(np.resize(levels, k // 32))).repeat(32)
    a = np.empty((k // 512, 16))
    for p in range(k // 512):
        a[p, :8] = np.random.permutation(np.resize(levels, 8))
        for g in range(8):
            far = levels[np.abs(levels - a[p, g]) >= 10]
            a[p, g + 8] = far[np.random.randint(len(far))]
    return np.exp2(a.ravel()).repeat(32)


BF16 = ml_dtypes.bfloat16


def bf(x):
    return np.asarray(x, np.float32).astype(BF16)


def f64(x):
    return np.asarray(x).astype(np.float64)


B, S, D, FF = 1, 512, 1024, 3072
T = B * S
EPS = 1e-5


def rms_rstd(u):
    return 1.0 / np.sqrt(np.square(u).mean(-1, keepdims=True) + EPS)


def setup_inputs():
    s = mx_kscale(T).reshape(B, S, 1)
    u = mx_kscale(D)
    v = mx_kscale(FF)
    c = 1.0 / (np.max(u) * np.max(s))
    h0 = bf(np.random.standard_normal((B, S, D)) * 1.3)
    w0 = bf(1.0 + 0.1 * np.random.standard_normal(D))
    wk0 = bf(np.random.standard_normal((D, FF)) / np.sqrt(D))
    wv0 = bf(np.random.standard_normal((FF, D)) / np.sqrt(FF))
    g = bf(np.random.standard_normal((B, S, D)) * np.exp2(np.random.randint(-6, 1, (B, S, 1))) / s * u * c)
    rstd = rms_rstd(f64(h0))
    z = (f64(h0) * rstd * f64(w0)) @ f64(wk0)
    return {"h_attn": bf(f64(h0) * s),
            "norm2_w": bf(f64(w0) * u),
            "ffn_wk": bf(f64(wk0) / v),
            "ffn_wv": bf(f64(wv0) * v[:, None] / u),
            "z": np.asarray(z, np.float32),
            "rstd": np.asarray(rstd, np.float32),
            "grad_out": g}


def reference(h_attn, norm2_w, ffn_wk, ffn_wv, z, rstd, grad_out):
    h = f64(h_attn).reshape(T, D)
    w = f64(norm2_w)
    r = f64(rstd).reshape(T, 1)
    zf = f64(z).reshape(T, FF)
    g = f64(grad_out).reshape(T, D)
    dk = mxq(g, 1, "e5m2") @ mxq(f64(ffn_wv), 1, "e4m3").T
    dz = dk * (2.0 * np.maximum(zf, 0.0))
    dhn = mxq(dz, 1, "e5m2") @ mxq(f64(ffn_wk), 1, "e4m3").T
    hn = h * r * w
    dwk = mxq(hn, 0, "e4m3").T @ mxq(dz, 0, "e5m2")
    n = dhn * w
    dh = g + r * n - h * (r * r * r) * (n * h).mean(-1, keepdims=True)
    return dh.reshape(B, S, D), dwk

@@ -1,0 +1,439 @@
+from contextlib import ExitStack
+
+import concourse.mybir as mybir
+from concourse.masks import make_identity
+
+T, D, FF = 512, 1024, 3072
+FLOPS = 3 * 2 * T * D * FF
+
+F32 = mybir.dt.float32
+BF16 = mybir.dt.bfloat16
+U32 = mybir.dt.uint32
+U8 = mybir.dt.uint8
+E4M3 = mybir.dt.float8_e4m3fn_x4
+E5M2 = mybir.dt.float8_e5m2_x4
+ALU = mybir.AluOpType
+ACT = mybir.ActivationFunctionType
+
+P = 128
+N = 512
+CHUNKS = FF // N
+H_AT = 0
+HN_AT = [0.5, 1, 1.5, 2]
+RAW_BUFS = 6
+O1_BUFS = 4
+LAG = 3
+O1_A = [0, 0, 0, 0, 0, 8]
+O1_B = [0, 0, 0, 0, 0, 0]
+O1_C = [8, 8, 8, 8]
+Z_BUFS = 4
+DZT_BUFS = 3
+WARM = 0
+WARM_MID = 0
+HN_IL_ACT = 0
+IL_ACT = []
+G_C = 0
+
+
+def tile_block_pc_v_kernel(tc, h_attn, norm2_w, ffn_wk, ffn_wv, z, rstd, grad_out, out_0, out_1):
+    nc = tc.nc
+    h_rows = h_attn.rearrange("b (p j) d -> p (b j) d", j=4)
+    g_rows = grad_out.rearrange("b (p j) d -> p (b j) d", j=4)
+    z_rows = z.rearrange("b (p j) f -> p (b j) f", j=4)
+    out0_rows = out_0.rearrange("b (p j) d -> p (b j) d", j=4)
+
+    with ExitStack() as ctx:
+        keep = ctx.enter_context(tc.tile_pool(name="keep", bufs=1))
+        ring = ctx.enter_context(tc.tile_pool(name="ring", bufs=2))
+        psum = ctx.enter_context(tc.psum_pool(name="psum", bufs=1))
+        ctx.enter_context(tc.manual_schedule())
+
+        rotation = list(range(8))
+
+        def bank(shape, fixed=None):
+            if fixed is None:
+                fixed = rotation[0]
+                rotation.remove(fixed)
+                rotation.append(fixed)
+            return psum.tile(shape, F32, name="bank%d" % fixed, tag="bank%d" % fixed)
+
+        def operand(pool, name, width, **kw):
+            codes = pool.tile([P, width], U32, name=name + "_codes", align_bytes=64, **kw)
+            scales = pool.tile([P, width], U8, name=name + "_scales", align_bytes=64, **kw)
+            return codes, scales
+
+        def quantize(op, staged, fmt):
+            nc.vector.quantize_mx(out=op[0][:].bitcast(fmt), scales=op[1][:], in_=staged)
+
+        def mm(acc, lhs, lhs_fmt, m0, rhs, rhs_fmt, start, stop):
+            nc.tensor.matmul_mx(
+                out=acc[:],
+                lhsT=lhs[0][:, m0 : m0 + P].bitcast(lhs_fmt),
+                lhsT_scale=lhs[1][:, m0 : m0 + P],
+                rhs=rhs[0][:].bitcast(rhs_fmt),
+                rhs_scale=rhs[1][:],
+                start=start,
+                stop=stop,
+            )
+
+        def load_pair(pool, name, src, **kw):
+            raw = pool.tile([P, 2, D], BF16, name=name, **kw)
+            nc.sync.dma_start(out=raw[:], in_=src)
+            return raw
+
+        stream = [("wv", 0, 0), ("wv", 0, 1)]
+        for f in range(CHUNKS):
+            if f + 1 < CHUNKS:
+                stream.extend([("wv", f + 1, 0), ("wv", f + 1, 1)])
+            stream.append(("z", f, 0))
+            if f >= LAG:
+                stream.append(("z", f - LAG, 1))
+            stream.extend([("wk", f, 0), ("wk", f, 1)])
+            if f == 0:
+                stream.append(("r", 0, 0))
+            if f == H_AT:
+                stream.extend([("h", 0, 0), ("h", 0, 1)])
+        stream.extend([("z", f, 1) for f in range(CHUNKS - LAG, CHUNKS)])
+        raw, used, in_ring, h_raw = {}, set(), {"w": [], "z": []}, []
+
+        def load(item):
+            kind, f, i = item
+            if kind == "r":
+                nc.sync.dma_start(out=r_cols[:], in_=rstd.rearrange("b (p j) o -> p (b j o)", j=4))
+            elif kind == "h":
+                h_raw.append(load_pair(keep, "h_raw%d" % i, h_rows[:, 2 * i : 2 * i + 2, :]))
+            elif kind == "z":
+                raw[item] = ring.tile([P, 2, N], F32, name="z_pair", tag="z", bufs=Z_BUFS)
+                nc.sync.dma_start(out=raw[item][:], in_=z_rows[:, 2 * i : 2 * i + 2, f * N : (f + 1) * N])
+            else:
+                if kind == "wv":
+                    rows = ffn_wv[f * N : (f + 1) * N, :].rearrange("(p r) k -> p r k", r=4)
+                else:
+                    q, half = divmod(f, 2)
+                    rows = ffn_wk[half * N : (half + 1) * N, q * D : (q + 1) * D].rearrange("(r p) k -> p r k", p=P)
+                raw[item] = load_pair(ring, "raw", rows[:, 2 * i : 2 * i + 2, :], bufs=RAW_BUFS)
+
+        waiting = []
+
+        def flush(keep_back):
+            while len(waiting) > keep_back:
+                dst, res = waiting[0]
+                nc.sync.dma_start(out=dst, in_=res[:])
+                waiting[:] = waiting[1:]
+
+        def prefetch(done):
+            for item in done:
+                used.add(item)
+            while stream:
+                item = stream[0]
+                if item[0] in ("wv", "wk", "z"):
+                    slots, depth = (in_ring["z"], Z_BUFS) if item[0] == "z" else (in_ring["w"], RAW_BUFS)
+                    if len(slots) >= depth and slots[len(slots) - depth] not in used:
+                        return
+                    slots.append(item)
+                load(item)
+                stream.remove(item)
+            flush(0)
+
+        def turn_weight(kind, f, order):
+            items = [(kind, f, i) for i in range(2)]
+            staged = turn([raw[item] for item in items], order)
+            prefetch(items)
+            return staged
+
+        def copy_turned(dst, turned, order):
+            if order == "slot major":
+                nc.scalar.copy(out=dst.rearrange("p (e c u) -> p e c u", e=2, u=2), in_=turned[:].rearrange("p e u c -> p e c u"))
+            else:
+                nc.scalar.copy(out=dst.rearrange("p (c e u) -> p c e u", e=2, u=2), in_=turned[:].rearrange("p e u c -> p c e u"))
+
+        def turn(raws, order):
+            staged = [ring.tile([P, 4 * N], BF16, name="staged", tag="staged", bufs=4, align_bytes=64) for g in range(2)]
+            for i in range(2):
+                words = raws[i][:].bitcast(F32)
+                for g in range(2):
+                    turned = bank([P, 2, 2, P])
+                    for e in range(2):
+                        for u in range(2):
+                            nc.tensor.transpose(turned[:, e, u, :], words[:, e, 256 * g + u : 256 * (g + 1) : 2], ident[:])
+                    copy_turned(staged[g][:].bitcast(F32)[:, i * N : (i + 1) * N], turned, order)
+            return staged
+
+        ident = keep.tile([P, P], F32, name="ident")
+        make_identity(nc, ident[:])
+
+        wv_op, wk_op, dz_tok, dz_feat, dz_bf = {}, {}, {}, {}, {}
+        w_cols = keep.tile([P, 8], BF16, name="w_cols")
+        nc.sync.dma_start(out=w_cols[:], in_=norm2_w.rearrange("(p j) -> p j", j=8))
+        g_raw = [load_pair(keep, "g_raw%d" % i, g_rows[:, 2 * i : 2 * i + 2, :]) for i in range(2)]
+        r_cols = keep.tile([P, 4], F32, name="r_cols")
+        prefetch([])
+
+        if WARM + WARM_MID:
+            warm_src = keep.tile([P, N], BF16, name="warm_src")
+
+        def warm(count):
+            if count:
+                junk = bank([P, N])
+                for i in range(count):
+                    nc.tensor.matmul(junk[:], lhsT=warm_src[:, 0:P], rhs=warm_src[:], start=True, stop=True)
+
+        if WARM + WARM_MID:
+            nc.vector.memset(warm_src[:], 0.0)
+        warm(WARM)
+
+        w_bank = bank([P, 4, P])
+        w_words = w_cols[:].bitcast(F32)
+        for j in range(4):
+            nc.tensor.transpose(w_bank[:, j, :], w_words[:, j : j + 1].to_broadcast([P, P]), ident[:])
+        w_row = keep.tile([P, D], BF16, name="w_row")
+        nc.scalar.copy(out=w_row[:].bitcast(F32).rearrange("p (c j) -> p c j", j=4), in_=w_bank[:].rearrange("p j c -> p c j"))
+
+        g_op = [operand(keep, "g%d" % g, N) for g in range(2)]
+        staged = turn(g_raw, "slot major")
+        for g in range(2):
+            quantize(g_op[g], staged[g][:], E5M2)
+        warm(WARM_MID)
+
+        def quantize_wv(f, staged):
+            wv_op[f] = [operand(ring, "wv", N, bufs=2 * LAG + 4) for g in range(2)]
+            for g in range(2):
+                quantize(wv_op[f][g], staged[g][:], E4M3)
+
+        def quantize_wk(unit, staged):
+            q, half = divmod(unit, 2)
+            for g in range(2):
+                wk_op[2 * q + g, half] = operand(keep, "wk%d_%d" % (2 * q + g, half), N)
+                quantize(wk_op[2 * q + g, half], staged[g][:], E4M3)
+
+        dk_acc = {}
+
+        def dk(f, t):
+            dk_acc[f, t] = bank([P, N])
+            for g in range(2):
+                mm(dk_acc[f, t], g_op[g], E5M2, t * P, wv_op[f][g], E4M3, g == 0, g == 1)
+
+        def dz(f, t):
+            acc = dk_acc[f, t]
+            z_view = raw["z", f, t // 2][:, t % 2, :].rearrange("p (w u e) -> p u w e", u=2, e=2)
+            for u in range(2):
+                cols = slice(u * 256, (u + 1) * 256)
+                nc.vector.scalar_tensor_tensor(
+                    out=dz_bf[f][:, t, cols].rearrange("p (w e) -> p w e", e=2),
+                    in0=z_view[:, u, :, :],
+                    scalar=0.0,
+                    in1=acc[:, cols].rearrange("p (w e) -> p w e", e=2),
+                    op0=ALU.max,
+                    op1=ALU.mult,
+                )
+            if t % 2:
+                prefetch([("z", f, t // 2)])
+
+        def turn_dz(f, pair):
+            staged = ring.tile([P, 2 * N], BF16, name="staged_dz", tag="staged_dz", bufs=3, align_bytes=64)
+            words = dz_bf[f][:].bitcast(F32)
+            turned = bank([P, 2, 2, P])
+            for e in range(2):
+                for u in range(2):
+                    nc.tensor.transpose(turned[:, e, u, :], words[:, 2 * pair + e, u * P : (u + 1) * P], ident[:])
+            copy_turned(staged[:].bitcast(F32), turned, "slot major")
+            return staged
+
+        def quantize_dz_feat(f, pair, staged):
+            dz_feat[f, pair] = operand(keep, "dzf%d_%d" % (f, pair), 256)
+            quantize(dz_feat[f, pair], staged[:], E5M2)
+
+        def interleave(dst, src, on_act):
+            dst = dst.rearrange("p (c i t) -> p c t i", i=4, t=4)
+            src = src.rearrange("p t (c i) -> p c t i", i=4)
+            if on_act:
+                nc.scalar.copy(out=dst, in_=src)
+            else:
+                nc.vector.tensor_copy(out=dst, in_=src)
+
+        hn_op = operand(keep, "hn", D)
+        r2_cols = keep.tile([P, 4], F32, name="r2_cols")
+        rr_cols = keep.tile([P, 4], F32, name="rr_cols")
+        hn_state = {}
+
+        def hn_part(j):
+            if j == 0:
+                hn_state["bf"] = ring.tile([P, 4, D], BF16, name="hn_bf", tag="o1", bufs=O1_BUFS, align_bytes=64)
+            nc.vector.scalar_tensor_tensor(
+                out=hn_state["bf"][:, j, :], in0=h_raw[j // 2][:, j % 2, :], scalar=r_cols[:, j : j + 1], in1=w_row[:],
+                op0=ALU.mult, op1=ALU.mult,
+            )
+
+        def hn_interleave():
+            hn_state["il"] = ring.tile([P, 4 * D], BF16, name="hn_il", tag="o1", bufs=O1_BUFS, align_bytes=64)
+            interleave(hn_state["il"][:], hn_state["bf"][:], HN_IL_ACT)
+
+        o1_sb = {}
+
+        def out1_tile(f, n):
+            half = n // 4
+            if n % 4 == 0:
+                o1_sb[f, half] = ring.tile([P, 4, N], F32, name="o1", tag="o1", bufs=O1_BUFS, align_bytes=64)
+            res = o1_sb[f, half]
+            acc = bank([P, N])
+            mm(acc, hn_op, E4M3, n * P, dz_tok[f], E5M2, True, True)
+            dst = res[:, n % 4, :].rearrange("p (w u e) -> p w u e", u=2, e=2)
+            src = acc[:].rearrange("p (u w e) -> p w u e", u=2, e=2)
+            nc.scalar.activation(out=dst, in_=src, func=ACT.Copy, scale=2.0)
+            if n % 4 == 3:
+                dst = out_1[half * N : (half + 1) * N, f * N : (f + 1) * N].rearrange("(n p) c -> p n c", p=P)
+                waiting.append((dst, res))
+                flush(O1_BUFS - 1 if stream else 0)
+
+        halves = [slice(0, N), slice(N, D)]
+        dhn_acc, dhn_bank, a_sb, res_sb = {}, {}, {}, {}
+
+        def dhn_pass(t, half, f):
+            if f == 0:
+                dhn_bank[t, half] = rotation[0]
+                dhn_acc[t, half] = bank([P, N])
+                rotation.remove(dhn_bank[t, half])
+            mm(dhn_acc[t, half], dz_feat[f, t // 2], E5M2, (t % 2) * P, wk_op[f, half], E4M3, f == 0, f == CHUNKS - 1)
+
+        o1_todo = [(f, n) for f in range(CHUNKS) for n in range(8)]
+
+        def weave(count, passes):
+            share = (len(passes) + count - 1) // max(count, 1)
+            for n in range(count):
+                out1_tile(*o1_todo[0])
+                o1_todo.remove(o1_todo[0])
+                for item in passes[n * share : (n + 1) * share]:
+                    dhn_pass(*item)
+            if count == 0:
+                for item in passes:
+                    dhn_pass(*item)
+
+        def dhn_read(t):
+            a_sb[t] = ring.tile([P, D], F32, name="a", tag="a", bufs=2)
+            for half in range(2):
+                nc.vector.scalar_tensor_tensor(
+                    out=a_sb[t][:, halves[half]], in0=dhn_acc[t, half][:], scalar=r2_cols[:, t : t + 1],
+                    in1=w_row[:, halves[half]], op0=ALU.mult, op1=ALU.mult,
+                )
+                rotation.append(dhn_bank[t, half])
+            res_sb[t] = ring.tile([P, D], F32, name="res", tag="res", bufs=2)
+            if G_C:
+                for half in range(2):
+                    nc.gpsimd.tensor_tensor(
+                        out=res_sb[t][:, halves[half]], in0=a_sb[t][:, halves[half]],
+                        in1=g_raw[t // 2][:, t % 2, halves[half]], op=ALU.add,
+                    )
+
+        def finish_out0(t):
+            a = a_sb[t]
+            res = res_sb[t]
+            spare = ring.tile([P, D], BF16, name="spare", tag="staged_dz", bufs=3, align_bytes=64)
+            coef = ring.tile([P, 1], F32, name="coef", bufs=2)
+            h_t = h_raw[t // 2][:, t % 2, :]
+            g_t = g_raw[t // 2][:, t % 2, :]
+            nc.vector.scalar_tensor_tensor(
+                out=spare[:], in0=a[:], scalar=rr_cols[:, t : t + 1], in1=h_t, op0=ALU.mult, op1=ALU.mult, accum_out=coef[:],
+            )
+            if not G_C:
+                nc.vector.tensor_tensor(out=res[:], in0=a[:], in1=g_t, op=ALU.add)
+            for half in range(2):
+                nc.vector.scalar_tensor_tensor(
+                    out=res[:, halves[half]], in0=h_t[:, halves[half]], scalar=coef[:], in1=res[:, halves[half]],
+                    op0=ALU.mult, op1=ALU.add,
+                )
+            nc.sync.dma_start(out=out0_rows[:, t, :], in_=res[:])
+
+        def token_side(f):
+            il = ring.tile([P, 4 * N], BF16, name="il", tag="staged", bufs=4, align_bytes=64)
+            interleave(il[:], dz_bf[f][:], f in IL_ACT)
+            return il
+
+        def quantize_tok(f, il):
+            dz_tok[f] = operand(ring, "dzt", N, bufs=DZT_BUFS)
+            quantize(dz_tok[f], il[:], E5M2)
+
+        quantize_wv(0, turn_weight("wv", 0, "row major"))
+
+        last = CHUNKS - 1
+        staged_dz = {}
+
+        def both(f, t):
+            dk(f, t)
+            dz(f, t)
+
+        def feat(f, pair):
+            quantize_dz_feat(f, pair, staged_dz[f, pair])
+
+        for f in range(CHUNKS):
+            late = f - LAG
+            if f < last:
+                staged_wv = turn_weight("wv", f + 1, "row major")
+            weave(O1_A[f], [])
+            dz_bf[f] = ring.tile([P, 4, N], BF16, name="dz_bf", bufs=LAG + 2)
+            both(f, 0)
+            if late >= 0:
+                both(late, 2)
+            if f < last:
+                quantize_wv(f + 1, staged_wv)
+            if f in HN_AT:
+                hn_part(HN_AT.index(f))
+            staged_wk = turn_weight("wk", f, "slot major")
+            weave(O1_B[f], [])
+            if late >= 0:
+                both(late, 3)
+            both(f, 1)
+            if late >= 0:
+                il = token_side(late)
+            quantize_wk(f, staged_wk)
+            if late >= 0:
+                quantize_tok(late, il)
+            if f == HN_AT[3]:
+                hn_interleave()
+            if f > 0:
+                staged_dz[f - 1, 0] = turn_dz(f - 1, 0)
+                feat(f - 1, 0)
+            if late > 0:
+                staged_dz[late - 1, 1] = turn_dz(late - 1, 1)
+                feat(late - 1, 1)
+            if f == HN_AT[3]:
+                quantize(hn_op, hn_state["il"][:], E4M3)
+                nc.vector.tensor_scalar(out=r2_cols[:], in0=r_cols[:], scalar1=2.0, scalar2=None, op0=ALU.mult)
+                nc.vector.scalar_tensor_tensor(
+                    out=rr_cols[:], in0=r_cols[:], scalar=-1.0 / D, in1=r_cols[:], op0=ALU.mult, op1=ALU.mult
+                )
+            for j in range(4):
+                if HN_AT[j] == f + 0.5:
+                    hn_part(j)
+
+        def passes(t, chunks):
+            return [(t, half, f) for half in range(2) for f in chunks]
+
+        every = list(range(CHUNKS))
+        staged_dz[last, 0] = turn_dz(last, 0)
+        for s in range(LAG):
+            c = CHUNKS - LAG + s
+            dk(c, 2)
+            dk(c, 3)
+            staged_dz[c - 1, 1] = turn_dz(c - 1, 1)
+            if s > 0:
+                dhn_read(s - 1)
+            dz(c, 2)
+            dz(c, 3)
+            if s == 0:
+                feat(last, 0)
+            feat(c - 1, 1)
+            il = token_side(c)
+            if c == last:
+                staged_dz[last, 1] = turn_dz(last, 1)
+                feat(last, 1)
+            quantize_tok(c, il)
+            weave(O1_C[s], passes(s, every))
+            if s > 0:
+                finish_out0(s - 1)
+        for s in range(LAG, 4):
+            dhn_read(s - 1)
+            weave(O1_C[s], passes(s, every))
+            finish_out0(s - 1)
+        dhn_read(3)
+        weave(len(o1_todo), [])
+        finish_out0(3)

@@ -18,21 +18,22 @@ ACT = mybir.ActivationFunctionType
 P = 128
 N = 512
 CHUNKS = FF // N
-H_AT = 0
-HN_AT = [0.5, 1, 1.5, 2]
 RAW_BUFS = 6
-O1_BUFS = 4
-LAG = 3
-O1_A = [0, 0, 0, 0, 0, 8]
-O1_B = [0, 0, 0, 0, 0, 0]
-O1_C = [8, 8, 8, 8]
+O1_BUFS = 5
+FULL = 4
+DZ_BUFS = 3
+WV_BUFS = 6
+O1_A = [0, 0, 0, 2, 4, 4]
+O1_B = [0, 0, 0, 2, 4, 4]
+O1_C = [8, 8, 8, 4]
 Z_BUFS = 4
-DZT_BUFS = 3
-WARM = 0
-WARM_MID = 0
+DZT_BUFS = 5
+WARM = 7
+WARM_MID = 1
 HN_IL_ACT = 0
 IL_ACT = []
 G_C = 0
+V_O1 = [(k // 8, k % 8) for k in (5, 7, 9, 11, 13, 15, 17, 19)]
 
 
 def tile_block_pc_v_kernel(tc, h_attn, norm2_w, ffn_wk, ffn_wv, z, rstd, grad_out, out_0, out_1):
@@ -86,14 +87,11 @@ def tile_block_pc_v_kernel(tc, h_attn, norm2_w, ffn_wk, ffn_wv, z, rstd, grad_ou
             if f + 1 < CHUNKS:
                 stream.extend([("wv", f + 1, 0), ("wv", f + 1, 1)])
             stream.append(("z", f, 0))
-            if f >= LAG:
-                stream.append(("z", f - LAG, 1))
-            stream.extend([("wk", f, 0), ("wk", f, 1)])
-            if f == 0:
-                stream.append(("r", 0, 0))
-            if f == H_AT:
-                stream.extend([("h", 0, 0), ("h", 0, 1)])
-        stream.extend([("z", f, 1) for f in range(CHUNKS - LAG, CHUNKS)])
+            stream.append(("wk", f, 0))
+            if f < FULL:
+                stream.append(("z", f, 1))
+            stream.append(("wk", f, 1))
+        stream.extend([("z", f, 1) for f in range(FULL, CHUNKS)])
         raw, used, in_ring, h_raw = {}, set(), {"w": [], "z": []}, []
 
         def load(item):
@@ -135,9 +133,9 @@ def tile_block_pc_v_kernel(tc, h_attn, norm2_w, ffn_wk, ffn_wv, z, rstd, grad_ou
                 stream.remove(item)
             flush(0)
 
-        def turn_weight(kind, f, order):
+        def turn_weight(kind, f, order, filler=0):
             items = [(kind, f, i) for i in range(2)]
-            staged = turn([raw[item] for item in items], order)
+            staged = turn([raw[item] for item in items], order, filler)
             prefetch(items)
             return staged
 
@@ -147,7 +145,7 @@ def tile_block_pc_v_kernel(tc, h_attn, norm2_w, ffn_wk, ffn_wv, z, rstd, grad_ou
             else:
                 nc.scalar.copy(out=dst.rearrange("p (c e u) -> p c e u", e=2, u=2), in_=turned[:].rearrange("p e u c -> p c e u"))
 
-        def turn(raws, order):
+        def turn(raws, order, filler=0):
             staged = [ring.tile([P, 4 * N], BF16, name="staged", tag="staged", bufs=4, align_bytes=64) for g in range(2)]
             for i in range(2):
                 words = raws[i][:].bitcast(F32)
@@ -157,6 +155,7 @@ def tile_block_pc_v_kernel(tc, h_attn, norm2_w, ffn_wk, ffn_wv, z, rstd, grad_ou
                         for u in range(2):
                             nc.tensor.transpose(turned[:, e, u, :], words[:, e, 256 * g + u : 256 * (g + 1) : 2], ident[:])
                     copy_turned(staged[g][:].bitcast(F32)[:, i * N : (i + 1) * N], turned, order)
+                warm(filler)
             return staged
 
         ident = keep.tile([P, P], F32, name="ident")
@@ -165,22 +164,18 @@ def tile_block_pc_v_kernel(tc, h_attn, norm2_w, ffn_wk, ffn_wv, z, rstd, grad_ou
         wv_op, wk_op, dz_tok, dz_feat, dz_bf = {}, {}, {}, {}, {}
         w_cols = keep.tile([P, 8], BF16, name="w_cols")
         nc.sync.dma_start(out=w_cols[:], in_=norm2_w.rearrange("(p j) -> p j", j=8))
-        g_raw = [load_pair(keep, "g_raw%d" % i, g_rows[:, 2 * i : 2 * i + 2, :]) for i in range(2)]
         r_cols = keep.tile([P, 4], F32, name="r_cols")
+        load(("r", 0, 0))
+        load(("h", 0, 0))
+        load(("h", 0, 1))
+        g_raw = [load_pair(keep, "g_raw%d" % i, g_rows[:, 2 * i : 2 * i + 2, :]) for i in range(2)]
         prefetch([])
-
-        if WARM + WARM_MID:
-            warm_src = keep.tile([P, N], BF16, name="warm_src")
 
         def warm(count):
             if count:
                 junk = bank([P, N])
                 for i in range(count):
-                    nc.tensor.matmul(junk[:], lhsT=warm_src[:, 0:P], rhs=warm_src[:], start=True, stop=True)
-
-        if WARM + WARM_MID:
-            nc.vector.memset(warm_src[:], 0.0)
-        warm(WARM)
+                    nc.tensor.matmul(junk[:], lhsT=h_raw[0][:, 0, 0:P], rhs=h_raw[0][:, 0, 0:N], start=True, stop=True)
 
         w_bank = bank([P, 4, P])
         w_words = w_cols[:].bitcast(F32)
@@ -190,13 +185,9 @@ def tile_block_pc_v_kernel(tc, h_attn, norm2_w, ffn_wk, ffn_wv, z, rstd, grad_ou
         nc.scalar.copy(out=w_row[:].bitcast(F32).rearrange("p (c j) -> p c j", j=4), in_=w_bank[:].rearrange("p j c -> p c j"))
 
         g_op = [operand(keep, "g%d" % g, N) for g in range(2)]
-        staged = turn(g_raw, "slot major")
-        for g in range(2):
-            quantize(g_op[g], staged[g][:], E5M2)
-        warm(WARM_MID)
 
         def quantize_wv(f, staged):
-            wv_op[f] = [operand(ring, "wv", N, bufs=2 * LAG + 4) for g in range(2)]
+            wv_op[f] = [operand(ring, "wv", N, bufs=WV_BUFS) for g in range(2)]
             for g in range(2):
                 quantize(wv_op[f][g], staged[g][:], E4M3)
 
@@ -279,7 +270,10 @@ def tile_block_pc_v_kernel(tc, h_attn, norm2_w, ffn_wk, ffn_wv, z, rstd, grad_ou
             mm(acc, hn_op, E4M3, n * P, dz_tok[f], E5M2, True, True)
             dst = res[:, n % 4, :].rearrange("p (w u e) -> p w u e", u=2, e=2)
             src = acc[:].rearrange("p (u w e) -> p w u e", u=2, e=2)
-            nc.scalar.activation(out=dst, in_=src, func=ACT.Copy, scale=2.0)
+            if (f, n) in V_O1:
+                nc.vector.tensor_scalar(out=dst, in0=src, scalar1=2.0, scalar2=None, op0=ALU.mult)
+            else:
+                nc.scalar.activation(out=dst, in_=src, func=ACT.Copy, scale=2.0)
             if n % 4 == 3:
                 dst = out_1[half * N : (half + 1) * N, f * N : (f + 1) * N].rearrange("(n p) c -> p n c", p=P)
                 waiting.append((dst, res))
@@ -352,7 +346,19 @@ def tile_block_pc_v_kernel(tc, h_attn, norm2_w, ffn_wk, ffn_wv, z, rstd, grad_ou
             dz_tok[f] = operand(ring, "dzt", N, bufs=DZT_BUFS)
             quantize(dz_tok[f], il[:], E5M2)
 
-        quantize_wv(0, turn_weight("wv", 0, "row major"))
+        warm(WARM)
+        for j in range(4):
+            hn_part(j)
+        staged = turn(g_raw, "slot major", WARM_MID)
+        for g in range(2):
+            quantize(g_op[g], staged[g][:], E5M2)
+        hn_interleave()
+        quantize_wv(0, turn_weight("wv", 0, "row major", WARM_MID))
+        quantize(hn_op, hn_state["il"][:], E4M3)
+        nc.vector.tensor_scalar(out=r2_cols[:], in0=r_cols[:], scalar1=2.0, scalar2=None, op0=ALU.mult)
+        nc.vector.scalar_tensor_tensor(
+            out=rr_cols[:], in0=r_cols[:], scalar=-1.0 / D, in1=r_cols[:], op0=ALU.mult, op1=ALU.mult
+        )
 
         last = CHUNKS - 1
         staged_dz = {}
@@ -365,63 +371,52 @@ def tile_block_pc_v_kernel(tc, h_attn, norm2_w, ffn_wk, ffn_wv, z, rstd, grad_ou
             quantize_dz_feat(f, pair, staged_dz[f, pair])
 
         for f in range(CHUNKS):
-            late = f - LAG
+            full = f < FULL
             if f < last:
-                staged_wv = turn_weight("wv", f + 1, "row major")
-            weave(O1_A[f], [])
-            dz_bf[f] = ring.tile([P, 4, N], BF16, name="dz_bf", bufs=LAG + 2)
+                staged_wv = turn_weight("wv", f + 1, "row major", WARM_MID if f == 0 else 0)
+            dz_bf[f] = ring.tile([P, 4, N], BF16, name="dz_bf", bufs=DZ_BUFS)
             both(f, 0)
-            if late >= 0:
-                both(late, 2)
+            if full:
+                both(f, 1)
+            weave(O1_A[f], [])
             if f < last:
                 quantize_wv(f + 1, staged_wv)
-            if f in HN_AT:
-                hn_part(HN_AT.index(f))
             staged_wk = turn_weight("wk", f, "slot major")
+            if full:
+                both(f, 2)
+                both(f, 3)
+            else:
+                both(f, 1)
             weave(O1_B[f], [])
-            if late >= 0:
-                both(late, 3)
-            both(f, 1)
-            if late >= 0:
-                il = token_side(late)
             quantize_wk(f, staged_wk)
-            if late >= 0:
-                quantize_tok(late, il)
-            if f == HN_AT[3]:
-                hn_interleave()
+            if full:
+                il = token_side(f)
             if f > 0:
-                staged_dz[f - 1, 0] = turn_dz(f - 1, 0)
-                feat(f - 1, 0)
-            if late > 0:
-                staged_dz[late - 1, 1] = turn_dz(late - 1, 1)
-                feat(late - 1, 1)
-            if f == HN_AT[3]:
-                quantize(hn_op, hn_state["il"][:], E4M3)
-                nc.vector.tensor_scalar(out=r2_cols[:], in0=r_cols[:], scalar1=2.0, scalar2=None, op0=ALU.mult)
-                nc.vector.scalar_tensor_tensor(
-                    out=rr_cols[:], in0=r_cols[:], scalar=-1.0 / D, in1=r_cols[:], op0=ALU.mult, op1=ALU.mult
-                )
-            for j in range(4):
-                if HN_AT[j] == f + 0.5:
-                    hn_part(j)
+                for pair in range(2 if f - 1 < FULL else 1):
+                    staged_dz[f - 1, pair] = turn_dz(f - 1, pair)
+                    feat(f - 1, pair)
+            if full:
+                quantize_tok(f, il)
 
         def passes(t, chunks):
             return [(t, half, f) for half in range(2) for f in chunks]
 
         every = list(range(CHUNKS))
+        lag = CHUNKS - FULL
         staged_dz[last, 0] = turn_dz(last, 0)
-        for s in range(LAG):
-            c = CHUNKS - LAG + s
+        for s in range(lag):
+            c = FULL + s
             dk(c, 2)
             dk(c, 3)
-            staged_dz[c - 1, 1] = turn_dz(c - 1, 1)
             if s > 0:
+                staged_dz[c - 1, 1] = turn_dz(c - 1, 1)
                 dhn_read(s - 1)
             dz(c, 2)
             dz(c, 3)
             if s == 0:
                 feat(last, 0)
-            feat(c - 1, 1)
+            else:
+                feat(c - 1, 1)
             il = token_side(c)
             if c == last:
                 staged_dz[last, 1] = turn_dz(last, 1)
@@ -430,7 +425,7 @@ def tile_block_pc_v_kernel(tc, h_attn, norm2_w, ffn_wk, ffn_wv, z, rstd, grad_ou
             weave(O1_C[s], passes(s, every))
             if s > 0:
                 finish_out0(s - 1)
-        for s in range(LAG, 4):
+        for s in range(lag, 4):
             dhn_read(s - 1)
             weave(O1_C[s], passes(s, every))
             finish_out0(s - 1)

@@ -13,35 +13,40 @@ U8 = mybir.dt.uint8
 E4M3 = mybir.dt.float8_e4m3fn_x4
 E5M2 = mybir.dt.float8_e5m2_x4
 ALU = mybir.AluOpType
-ACT = mybir.ActivationFunctionType
 
 P = 128
 N = 512
 CHUNKS = FF // N
-RAW_BUFS = 6
-O1_BUFS = 5
-FULL = 4
-DZ_BUFS = 3
-WV_BUFS = 6
-O1_A = [0, 0, 0, 2, 4, 4]
-O1_B = [0, 0, 0, 2, 4, 4]
-O1_C = [8, 8, 8, 4]
+LAST = CHUNKS - 1
+SLOTS = 4
+BANKS = 8
+ALIGN = 64
+
+LATE_CHUNKS = (LAST - 1, LAST)
+
+OUT1_PER_GAP = 3
+OUT1_PER_LATE_GAP = 2
+OUT1_PER_DHN = 6
+
+WARM_FIRST = 7
+
+WEIGHT_BUFS = 6
 Z_BUFS = 4
-DZT_BUFS = 5
-WARM = 7
-WARM_MID = 1
-HN_IL_ACT = 0
-IL_ACT = []
-G_C = 0
-V_O1 = [(k // 8, k % 8) for k in (5, 7, 9, 11, 13, 15, 17, 19)]
+STAGED_BUFS = 4
+HALF_STAGED_BUFS = 3
+OUT1_BUFS = 5
+WV_BUFS = 6
+DZ_BUFS = 3
+DZ_TOK_BUFS = 5
 
 
 def tile_block_pc_v_kernel(tc, h_attn, norm2_w, ffn_wk, ffn_wv, z, rstd, grad_out, out_0, out_1):
     nc = tc.nc
-    h_rows = h_attn.rearrange("b (p j) d -> p (b j) d", j=4)
-    g_rows = grad_out.rearrange("b (p j) d -> p (b j) d", j=4)
-    z_rows = z.rearrange("b (p j) f -> p (b j) f", j=4)
-    out0_rows = out_0.rearrange("b (p j) d -> p (b j) d", j=4)
+    h_rows = h_attn.rearrange("b (p t) d -> p (b t) d", t=SLOTS)
+    g_rows = grad_out.rearrange("b (p t) d -> p (b t) d", t=SLOTS)
+    z_rows = z.rearrange("b (p t) f -> p (b t) f", t=SLOTS)
+    out0_rows = out_0.rearrange("b (p t) d -> p (b t) d", t=SLOTS)
+    d_halves = [slice(0, N), slice(N, D)]
 
     with ExitStack() as ctx:
         keep = ctx.enter_context(tc.tile_pool(name="keep", bufs=1))
@@ -49,386 +54,362 @@ def tile_block_pc_v_kernel(tc, h_attn, norm2_w, ffn_wk, ffn_wv, z, rstd, grad_ou
         psum = ctx.enter_context(tc.psum_pool(name="psum", bufs=1))
         ctx.enter_context(tc.manual_schedule())
 
-        rotation = list(range(8))
+        rotation = list(range(BANKS))
 
-        def bank(shape, fixed=None):
-            if fixed is None:
-                fixed = rotation[0]
-                rotation.remove(fixed)
-                rotation.append(fixed)
-            return psum.tile(shape, F32, name="bank%d" % fixed, tag="bank%d" % fixed)
+        def next_bank(shape):
+            index = rotation[0]
+            rotation.remove(index)
+            rotation.append(index)
+            return psum.tile(shape, F32, name="bank%d" % index, tag="bank%d" % index)
 
-        def operand(pool, name, width, **kw):
-            codes = pool.tile([P, width], U32, name=name + "_codes", align_bytes=64, **kw)
-            scales = pool.tile([P, width], U8, name=name + "_scales", align_bytes=64, **kw)
-            return codes, scales
+        def quantize(pool, name, staged, fmt, **ring_depth):
+            width = staged.shape[1] // 4
+            codes = pool.tile([P, width], U32, name=name + "_codes", align_bytes=ALIGN, **ring_depth)
+            scales = pool.tile([P, width], U8, name=name + "_scales", align_bytes=ALIGN, **ring_depth)
+            nc.vector.quantize_mx(out=codes[:].bitcast(fmt), scales=scales[:], in_=staged[:])
+            return codes, scales, fmt
 
-        def quantize(op, staged, fmt):
-            nc.vector.quantize_mx(out=op[0][:].bitcast(fmt), scales=op[1][:], in_=staged)
-
-        def mm(acc, lhs, lhs_fmt, m0, rhs, rhs_fmt, start, stop):
+        def mx_pass(acc, stationary, first_column, moving, start, stop):
+            columns = slice(first_column, first_column + P)
             nc.tensor.matmul_mx(
                 out=acc[:],
-                lhsT=lhs[0][:, m0 : m0 + P].bitcast(lhs_fmt),
-                lhsT_scale=lhs[1][:, m0 : m0 + P],
-                rhs=rhs[0][:].bitcast(rhs_fmt),
-                rhs_scale=rhs[1][:],
+                lhsT=stationary[0][:, columns].bitcast(stationary[2]),
+                lhsT_scale=stationary[1][:, columns],
+                rhs=moving[0][:].bitcast(moving[2]),
+                rhs_scale=moving[1][:],
                 start=start,
                 stop=stop,
             )
 
-        def load_pair(pool, name, src, **kw):
-            raw = pool.tile([P, 2, D], BF16, name=name, **kw)
-            nc.sync.dma_start(out=raw[:], in_=src)
-            return raw
-
-        stream = [("wv", 0, 0), ("wv", 0, 1)]
+        stream = [("rstd", 0, 0), ("h", 0, 0), ("wv", 0, 0), ("wv", 0, 1), ("h", 0, 1)]
         for f in range(CHUNKS):
-            if f + 1 < CHUNKS:
+            if f < LAST:
                 stream.extend([("wv", f + 1, 0), ("wv", f + 1, 1)])
-            stream.append(("z", f, 0))
-            stream.append(("wk", f, 0))
-            if f < FULL:
+            stream.extend([("z", f, 0), ("wk", f, 0)])
+            if f not in LATE_CHUNKS:
                 stream.append(("z", f, 1))
             stream.append(("wk", f, 1))
-        stream.extend([("z", f, 1) for f in range(FULL, CHUNKS)])
-        raw, used, in_ring, h_raw = {}, set(), {"w": [], "z": []}, []
+        stream.extend([("z", f, 1) for f in LATE_CHUNKS])
+        loaded, consumed, held_stores = {}, set(), []
+        issued = {"weights": [], "z": []}
 
-        def load(item):
-            kind, f, i = item
-            if kind == "r":
-                nc.sync.dma_start(out=r_cols[:], in_=rstd.rearrange("b (p j) o -> p (b j o)", j=4))
-            elif kind == "h":
-                h_raw.append(load_pair(keep, "h_raw%d" % i, h_rows[:, 2 * i : 2 * i + 2, :]))
-            elif kind == "z":
-                raw[item] = ring.tile([P, 2, N], F32, name="z_pair", tag="z", bufs=Z_BUFS)
-                nc.sync.dma_start(out=raw[item][:], in_=z_rows[:, 2 * i : 2 * i + 2, f * N : (f + 1) * N])
+        def load_pair(pool, name, rows, pair, **ring_depth):
+            tile = pool.tile([P, 2, rows.shape[2]], rows.dtype, name=name, **ring_depth)
+            nc.sync.dma_start(out=tile[:], in_=rows[:, 2 * pair : 2 * pair + 2, :])
+            return tile
+
+        def load(kind, index, pair):
+            if kind == "rstd":
+                tile = keep.tile([P, SLOTS], F32, name="rstd")
+                nc.sync.dma_start(out=tile[:], in_=rstd.rearrange("b (p t) o -> p (b t o)", t=SLOTS))
+                return tile
+            if kind == "h":
+                return load_pair(keep, "h%d" % pair, h_rows, pair)
+            if kind == "z":
+                return load_pair(ring, "z", z_rows[:, :, index * N : (index + 1) * N], pair, bufs=Z_BUFS)
+            if kind == "wv":
+                rows = ffn_wv[index * N : (index + 1) * N, :].rearrange("(p r) k -> p r k", r=4)
             else:
-                if kind == "wv":
-                    rows = ffn_wv[f * N : (f + 1) * N, :].rearrange("(p r) k -> p r k", r=4)
-                else:
-                    q, half = divmod(f, 2)
-                    rows = ffn_wk[half * N : (half + 1) * N, q * D : (q + 1) * D].rearrange("(r p) k -> p r k", p=P)
-                raw[item] = load_pair(ring, "raw", rows[:, 2 * i : 2 * i + 2, :], bufs=RAW_BUFS)
+                chunk_pair, half = divmod(index, 2)
+                rows = ffn_wk[d_halves[half], chunk_pair * 2 * N : (chunk_pair + 1) * 2 * N]
+                rows = rows.rearrange("(r p) k -> p r k", p=P)
+            return load_pair(ring, "weight", rows, pair, bufs=WEIGHT_BUFS)
 
-        waiting = []
+        def issue_stores(keep_back):
+            while len(held_stores) > keep_back:
+                dst, tile = held_stores[0]
+                nc.sync.dma_start(out=dst, in_=tile[:])
+                held_stores[:] = held_stores[1:]
 
-        def flush(keep_back):
-            while len(waiting) > keep_back:
-                dst, res = waiting[0]
-                nc.sync.dma_start(out=dst, in_=res[:])
-                waiting[:] = waiting[1:]
-
-        def prefetch(done):
-            for item in done:
-                used.add(item)
+        def issue_loads(*just_read):
+            for item in just_read:
+                consumed.add(item)
             while stream:
                 item = stream[0]
                 if item[0] in ("wv", "wk", "z"):
-                    slots, depth = (in_ring["z"], Z_BUFS) if item[0] == "z" else (in_ring["w"], RAW_BUFS)
-                    if len(slots) >= depth and slots[len(slots) - depth] not in used:
+                    earlier, depth = (issued["z"], Z_BUFS) if item[0] == "z" else (issued["weights"], WEIGHT_BUFS)
+                    if len(earlier) >= depth and earlier[len(earlier) - depth] not in consumed:
                         return
-                    slots.append(item)
-                load(item)
+                    earlier.append(item)
+                loaded[item] = load(*item)
                 stream.remove(item)
-            flush(0)
+            issue_stores(0)
 
-        def turn_weight(kind, f, order, filler=0):
-            items = [(kind, f, i) for i in range(2)]
-            staged = turn([raw[item] for item in items], order, filler)
-            prefetch(items)
+        def copy_turned(dst_words, turned, column_order):
+            nc.scalar.copy(
+                out=dst_words.rearrange("p (%s u) -> p %s u" % (column_order, column_order), e=2, u=2),
+                in_=turned[:].rearrange("p e u c -> p %s u" % column_order),
+            )
+
+        def new_staged():
+            return [
+                ring.tile([P, 4 * N], BF16, name="staged", tag="staged", bufs=STAGED_BUFS, align_bytes=ALIGN)
+                for k_pass in range(2)
+            ]
+
+        def turn_pair(source, pair, staged, column_order):
+            words = source[:].bitcast(F32)
+            for k_pass in range(2):
+                turned = next_bank([P, 2, 2, P])
+                for e in range(2):
+                    for u in range(2):
+                        every_second = words[:, e, 256 * k_pass + u : 256 * (k_pass + 1) : 2]
+                        nc.tensor.transpose(turned[:, e, u, :], every_second, identity[:])
+                copy_turned(staged[k_pass][:].bitcast(F32)[:, pair * N : (pair + 1) * N], turned, column_order)
+
+        def turn_weight(kind, index, column_order, keep_warm):
+            staged = new_staged()
+            for pair in range(2):
+                turn_pair(loaded[kind, index, pair], pair, staged, column_order)
+                if keep_warm:
+                    warm(1)
+            issue_loads((kind, index, 0), (kind, index, 1))
             return staged
 
-        def copy_turned(dst, turned, order):
-            if order == "slot major":
-                nc.scalar.copy(out=dst.rearrange("p (e c u) -> p e c u", e=2, u=2), in_=turned[:].rearrange("p e u c -> p e c u"))
-            else:
-                nc.scalar.copy(out=dst.rearrange("p (c e u) -> p c e u", e=2, u=2), in_=turned[:].rearrange("p e u c -> p c e u"))
+        def interleave(name, source, **tile_options):
+            out = ring.tile([P, SLOTS * source.shape[2]], BF16, name=name, align_bytes=ALIGN, **tile_options)
+            nc.vector.tensor_copy(
+                out=out[:].rearrange("p (c i t) -> p c t i", i=4, t=SLOTS),
+                in_=source[:].rearrange("p t (c i) -> p c t i", i=4),
+            )
+            return out
 
-        def turn(raws, order, filler=0):
-            staged = [ring.tile([P, 4 * N], BF16, name="staged", tag="staged", bufs=4, align_bytes=64) for g in range(2)]
-            for i in range(2):
-                words = raws[i][:].bitcast(F32)
-                for g in range(2):
-                    turned = bank([P, 2, 2, P])
-                    for e in range(2):
-                        for u in range(2):
-                            nc.tensor.transpose(turned[:, e, u, :], words[:, e, 256 * g + u : 256 * (g + 1) : 2], ident[:])
-                    copy_turned(staged[g][:].bitcast(F32)[:, i * N : (i + 1) * N], turned, order)
-                warm(filler)
-            return staged
+        identity = keep.tile([P, P], F32, name="identity")
+        make_identity(nc, identity[:])
+        w_columns = keep.tile([P, 8], BF16, name="w_columns")
+        nc.sync.dma_start(out=w_columns[:], in_=norm2_w.rearrange("(p j) -> p j", j=8))
+        g_pairs = [load_pair(keep, "g%d" % pair, g_rows, pair) for pair in range(2)]
+        issue_loads()
 
-        ident = keep.tile([P, P], F32, name="ident")
-        make_identity(nc, ident[:])
-
-        wv_op, wk_op, dz_tok, dz_feat, dz_bf = {}, {}, {}, {}, {}
-        w_cols = keep.tile([P, 8], BF16, name="w_cols")
-        nc.sync.dma_start(out=w_cols[:], in_=norm2_w.rearrange("(p j) -> p j", j=8))
-        r_cols = keep.tile([P, 4], F32, name="r_cols")
-        load(("r", 0, 0))
-        load(("h", 0, 0))
-        load(("h", 0, 1))
-        g_raw = [load_pair(keep, "g_raw%d" % i, g_rows[:, 2 * i : 2 * i + 2, :]) for i in range(2)]
-        prefetch([])
+        zeros = keep.tile([P, N], BF16, name="zeros")
+        nc.vector.memset(zeros[:], 0.0)
 
         def warm(count):
-            if count:
-                junk = bank([P, N])
-                for i in range(count):
-                    nc.tensor.matmul(junk[:], lhsT=h_raw[0][:, 0, 0:P], rhs=h_raw[0][:, 0, 0:N], start=True, stop=True)
+            unread = next_bank([P, N])
+            for repeat in range(count):
+                nc.tensor.matmul(unread[:], lhsT=zeros[:, 0:P], rhs=zeros[:], start=True, stop=True)
 
-        w_bank = bank([P, 4, P])
-        w_words = w_cols[:].bitcast(F32)
+        warm(WARM_FIRST)
+
+        w_turned = next_bank([P, 4, P])
+        w_words = w_columns[:].bitcast(F32)
         for j in range(4):
-            nc.tensor.transpose(w_bank[:, j, :], w_words[:, j : j + 1].to_broadcast([P, P]), ident[:])
+            nc.tensor.transpose(w_turned[:, j, :], w_words[:, j : j + 1].to_broadcast([P, P]), identity[:])
         w_row = keep.tile([P, D], BF16, name="w_row")
-        nc.scalar.copy(out=w_row[:].bitcast(F32).rearrange("p (c j) -> p c j", j=4), in_=w_bank[:].rearrange("p j c -> p c j"))
+        nc.scalar.copy(
+            out=w_row[:].bitcast(F32).rearrange("p (c j) -> p c j", j=4),
+            in_=w_turned[:].rearrange("p j c -> p c j"),
+        )
 
-        g_op = [operand(keep, "g%d" % g, N) for g in range(2)]
+        def h_slot(t):
+            return loaded["h", 0, t // 2][:, t % 2, :]
+
+        wv_mx, wk_mx, dz_bf16, dz_tok_mx, dz_feat_mx = {}, {}, {}, {}, {}
 
         def quantize_wv(f, staged):
-            wv_op[f] = [operand(ring, "wv", N, bufs=WV_BUFS) for g in range(2)]
-            for g in range(2):
-                quantize(wv_op[f][g], staged[g][:], E4M3)
+            wv_mx[f] = [quantize(ring, "wv", staged[k_pass], E4M3, bufs=WV_BUFS) for k_pass in range(2)]
 
-        def quantize_wk(unit, staged):
-            q, half = divmod(unit, 2)
-            for g in range(2):
-                wk_op[2 * q + g, half] = operand(keep, "wk%d_%d" % (2 * q + g, half), N)
-                quantize(wk_op[2 * q + g, half], staged[g][:], E4M3)
+        def quantize_wk(index, staged):
+            chunk_pair, half = divmod(index, 2)
+            for k_pass in range(2):
+                f = 2 * chunk_pair + k_pass
+                wk_mx[f, half] = quantize(keep, "wk%d_%d" % (f, half), staged[k_pass], E4M3)
 
-        dk_acc = {}
-
-        def dk(f, t):
-            dk_acc[f, t] = bank([P, N])
-            for g in range(2):
-                mm(dk_acc[f, t], g_op[g], E5M2, t * P, wv_op[f][g], E4M3, g == 0, g == 1)
-
-        def dz(f, t):
-            acc = dk_acc[f, t]
-            z_view = raw["z", f, t // 2][:, t % 2, :].rearrange("p (w u e) -> p u w e", u=2, e=2)
+        def make_dz(f, t):
+            if t == 0:
+                dz_bf16[f] = ring.tile([P, SLOTS, N], BF16, name="dz_bf16", bufs=DZ_BUFS)
+            dk = next_bank([P, N])
+            for k_pass in range(2):
+                mx_pass(dk, g_mx[k_pass], t * P, wv_mx[f][k_pass], k_pass == 0, k_pass == 1)
+            z_view = loaded["z", f, t // 2][:, t % 2, :].rearrange("p (w u e) -> p u w e", u=2, e=2)
             for u in range(2):
-                cols = slice(u * 256, (u + 1) * 256)
+                columns = slice(u * 256, (u + 1) * 256)
                 nc.vector.scalar_tensor_tensor(
-                    out=dz_bf[f][:, t, cols].rearrange("p (w e) -> p w e", e=2),
+                    out=dz_bf16[f][:, t, columns].rearrange("p (w e) -> p w e", e=2),
                     in0=z_view[:, u, :, :],
                     scalar=0.0,
-                    in1=acc[:, cols].rearrange("p (w e) -> p w e", e=2),
+                    in1=dk[:, columns].rearrange("p (w e) -> p w e", e=2),
                     op0=ALU.max,
                     op1=ALU.mult,
                 )
             if t % 2:
-                prefetch([("z", f, t // 2)])
+                issue_loads(("z", f, t // 2))
 
         def turn_dz(f, pair):
-            staged = ring.tile([P, 2 * N], BF16, name="staged_dz", tag="staged_dz", bufs=3, align_bytes=64)
-            words = dz_bf[f][:].bitcast(F32)
-            turned = bank([P, 2, 2, P])
+            staged = ring.tile(
+                [P, 2 * N], BF16, name="staged_dz", tag="half_staged", bufs=HALF_STAGED_BUFS, align_bytes=ALIGN
+            )
+            words = dz_bf16[f][:].bitcast(F32)
+            turned = next_bank([P, 2, 2, P])
             for e in range(2):
                 for u in range(2):
-                    nc.tensor.transpose(turned[:, e, u, :], words[:, 2 * pair + e, u * P : (u + 1) * P], ident[:])
-            copy_turned(staged[:].bitcast(F32), turned, "slot major")
+                    nc.tensor.transpose(turned[:, e, u, :], words[:, 2 * pair + e, u * P : (u + 1) * P], identity[:])
+            copy_turned(staged[:].bitcast(F32), turned, "e c")
             return staged
 
         def quantize_dz_feat(f, pair, staged):
-            dz_feat[f, pair] = operand(keep, "dzf%d_%d" % (f, pair), 256)
-            quantize(dz_feat[f, pair], staged[:], E5M2)
+            dz_feat_mx[f, pair] = quantize(keep, "dz_feat%d_%d" % (f, pair), staged, E5M2)
 
-        def interleave(dst, src, on_act):
-            dst = dst.rearrange("p (c i t) -> p c t i", i=4, t=4)
-            src = src.rearrange("p t (c i) -> p c t i", i=4)
-            if on_act:
-                nc.scalar.copy(out=dst, in_=src)
-            else:
-                nc.vector.tensor_copy(out=dst, in_=src)
+        def interleave_dz(f):
+            return interleave("dz_interleaved", dz_bf16[f], tag="staged", bufs=STAGED_BUFS)
 
-        hn_op = operand(keep, "hn", D)
-        r2_cols = keep.tile([P, 4], F32, name="r2_cols")
-        rr_cols = keep.tile([P, 4], F32, name="rr_cols")
-        hn_state = {}
+        def quantize_dz_tok(f, staged):
+            dz_tok_mx[f] = quantize(ring, "dz_tok", staged, E5M2, bufs=DZ_TOK_BUFS)
 
-        def hn_part(j):
-            if j == 0:
-                hn_state["bf"] = ring.tile([P, 4, D], BF16, name="hn_bf", tag="o1", bufs=O1_BUFS, align_bytes=64)
+        out1_todo = [(f, n) for f in range(CHUNKS) for n in range(D // P)]
+        out1_sb = {}
+
+        def out1_tile():
+            f, n = out1_todo[0]
+            out1_todo.remove((f, n))
+            half, row = divmod(n, 4)
+            if row == 0:
+                out1_sb[f, half] = ring.tile([P, 4, N], F32, name="out1", tag="out1", bufs=OUT1_BUFS, align_bytes=ALIGN)
+            acc = next_bank([P, N])
+            mx_pass(acc, hn_mx, n * P, dz_tok_mx[f], True, True)
+            nc.scalar.copy(
+                out=out1_sb[f, half][:, row, :].rearrange("p (w u e) -> p w u e", u=2, e=2),
+                in_=acc[:].rearrange("p (u w e) -> p w u e", u=2, e=2),
+            )
+            if row == 3:
+                dst = out_1[d_halves[half], f * N : (f + 1) * N].rearrange("(n p) c -> p n c", p=P)
+                held_stores.append((dst, out1_sb[f, half]))
+                issue_stores(OUT1_BUFS - 1 if stream else 0)
+
+        def out1_tiles(count):
+            for repeat in range(count):
+                out1_tile()
+
+        def dhn_with_out1(t):
+            sums = []
+            for half in range(2):
+                for f in range(CHUNKS):
+                    if f % (2 * CHUNKS // OUT1_PER_DHN) == 0:
+                        out1_tile()
+                    if f == 0:
+                        index = rotation[0]
+                        sums.append((index, next_bank([P, N])))
+                        rotation.remove(index)
+                    mx_pass(sums[half][1], dz_feat_mx[f, t // 2], (t % 2) * P, wk_mx[f, half], f == 0, f == LAST)
+            return sums
+
+        def scale_dhn(t, sums):
+            rn = ring.tile([P, D], F32, name="rn", bufs=2)
+            for half in range(2):
+                index, acc = sums[half]
+                nc.vector.scalar_tensor_tensor(
+                    out=rn[:, d_halves[half]], in0=acc[:], scalar=two_rstd[:, t : t + 1], in1=w_row[:, d_halves[half]],
+                    op0=ALU.mult, op1=ALU.mult,
+                )
+                rotation.append(index)
+            return rn
+
+        def finish_out0(t, rn):
+            result = ring.tile([P, D], F32, name="result", bufs=2)
+            products = ring.tile(
+                [P, D], BF16, name="products", tag="half_staged", bufs=HALF_STAGED_BUFS, align_bytes=ALIGN
+            )
+            coef = ring.tile([P, 1], F32, name="coef", bufs=2)
+            g_slot = g_pairs[t // 2][:, t % 2, :]
+            low, high = d_halves
+            nc.vector.tensor_tensor(out=result[:, low], in0=rn[:, low], in1=g_slot[:, low], op=ALU.add)
             nc.vector.scalar_tensor_tensor(
-                out=hn_state["bf"][:, j, :], in0=h_raw[j // 2][:, j % 2, :], scalar=r_cols[:, j : j + 1], in1=w_row[:],
+                out=products[:], in0=rn[:], scalar=mean_factor[:, t : t + 1], in1=h_slot(t),
+                op0=ALU.mult, op1=ALU.mult, accum_out=coef[:],
+            )
+            nc.vector.tensor_tensor(out=result[:, high], in0=rn[:, high], in1=g_slot[:, high], op=ALU.add)
+            for columns in d_halves:
+                nc.vector.scalar_tensor_tensor(
+                    out=result[:, columns], in0=h_slot(t)[:, columns], scalar=coef[:], in1=result[:, columns],
+                    op0=ALU.mult, op1=ALU.add,
+                )
+                if t == SLOTS - 1:
+                    nc.sync.dma_start(out=out0_rows[:, t, columns], in_=result[:, columns])
+            if t < SLOTS - 1:
+                nc.sync.dma_start(out=out0_rows[:, t, :], in_=result[:])
+
+        staged_g = new_staged()
+        for pair in range(2):
+            turn_pair(g_pairs[pair], pair, staged_g, "e c")
+            warm(1)
+        g_mx = [quantize(keep, "g%d" % k_pass, staged_g[k_pass], E5M2) for k_pass in range(2)]
+
+        rstd_columns = loaded["rstd", 0, 0]
+        two_rstd = keep.tile([P, SLOTS], F32, name="two_rstd")
+        nc.vector.tensor_scalar(out=two_rstd[:], in0=rstd_columns[:], scalar1=2.0, scalar2=None, op0=ALU.mult)
+        mean_factor = keep.tile([P, SLOTS], F32, name="mean_factor")
+        nc.vector.scalar_tensor_tensor(
+            out=mean_factor[:], in0=rstd_columns[:], scalar=-1.0 / D, in1=rstd_columns[:], op0=ALU.mult, op1=ALU.mult
+        )
+        hn_bf16 = ring.tile([P, SLOTS, D], BF16, name="hn_bf16", tag="out1", bufs=OUT1_BUFS, align_bytes=ALIGN)
+
+        def make_hn(t):
+            nc.vector.scalar_tensor_tensor(
+                out=hn_bf16[:, t, :], in0=h_slot(t), scalar=two_rstd[:, t : t + 1], in1=w_row[:],
                 op0=ALU.mult, op1=ALU.mult,
             )
 
-        def hn_interleave():
-            hn_state["il"] = ring.tile([P, 4 * D], BF16, name="hn_il", tag="o1", bufs=O1_BUFS, align_bytes=64)
-            interleave(hn_state["il"][:], hn_state["bf"][:], HN_IL_ACT)
+        make_hn(0)
+        make_hn(1)
+        quantize_wv(0, turn_weight("wv", 0, "c e", True))
+        make_hn(2)
+        make_hn(3)
 
-        o1_sb = {}
-
-        def out1_tile(f, n):
-            half = n // 4
-            if n % 4 == 0:
-                o1_sb[f, half] = ring.tile([P, 4, N], F32, name="o1", tag="o1", bufs=O1_BUFS, align_bytes=64)
-            res = o1_sb[f, half]
-            acc = bank([P, N])
-            mm(acc, hn_op, E4M3, n * P, dz_tok[f], E5M2, True, True)
-            dst = res[:, n % 4, :].rearrange("p (w u e) -> p w u e", u=2, e=2)
-            src = acc[:].rearrange("p (u w e) -> p w u e", u=2, e=2)
-            if (f, n) in V_O1:
-                nc.vector.tensor_scalar(out=dst, in0=src, scalar1=2.0, scalar2=None, op0=ALU.mult)
-            else:
-                nc.scalar.activation(out=dst, in_=src, func=ACT.Copy, scale=2.0)
-            if n % 4 == 3:
-                dst = out_1[half * N : (half + 1) * N, f * N : (f + 1) * N].rearrange("(n p) c -> p n c", p=P)
-                waiting.append((dst, res))
-                flush(O1_BUFS - 1 if stream else 0)
-
-        halves = [slice(0, N), slice(N, D)]
-        dhn_acc, dhn_bank, a_sb, res_sb = {}, {}, {}, {}
-
-        def dhn_pass(t, half, f):
+        for f in range(LAST):
+            late = f in LATE_CHUNKS
+            per_gap = OUT1_PER_LATE_GAP if late else OUT1_PER_GAP
+            staged_wv = turn_weight("wv", f + 1, "c e", f == 0)
+            make_dz(f, 0)
+            if not late:
+                make_dz(f, 1)
+            if f > 1:
+                out1_tiles(per_gap)
+            quantize_wv(f + 1, staged_wv)
             if f == 0:
-                dhn_bank[t, half] = rotation[0]
-                dhn_acc[t, half] = bank([P, N])
-                rotation.remove(dhn_bank[t, half])
-            mm(dhn_acc[t, half], dz_feat[f, t // 2], E5M2, (t % 2) * P, wk_op[f, half], E4M3, f == 0, f == CHUNKS - 1)
-
-        o1_todo = [(f, n) for f in range(CHUNKS) for n in range(8)]
-
-        def weave(count, passes):
-            share = (len(passes) + count - 1) // max(count, 1)
-            for n in range(count):
-                out1_tile(*o1_todo[0])
-                o1_todo.remove(o1_todo[0])
-                for item in passes[n * share : (n + 1) * share]:
-                    dhn_pass(*item)
-            if count == 0:
-                for item in passes:
-                    dhn_pass(*item)
-
-        def dhn_read(t):
-            a_sb[t] = ring.tile([P, D], F32, name="a", tag="a", bufs=2)
-            for half in range(2):
-                nc.vector.scalar_tensor_tensor(
-                    out=a_sb[t][:, halves[half]], in0=dhn_acc[t, half][:], scalar=r2_cols[:, t : t + 1],
-                    in1=w_row[:, halves[half]], op0=ALU.mult, op1=ALU.mult,
-                )
-                rotation.append(dhn_bank[t, half])
-            res_sb[t] = ring.tile([P, D], F32, name="res", tag="res", bufs=2)
-            if G_C:
-                for half in range(2):
-                    nc.gpsimd.tensor_tensor(
-                        out=res_sb[t][:, halves[half]], in0=a_sb[t][:, halves[half]],
-                        in1=g_raw[t // 2][:, t % 2, halves[half]], op=ALU.add,
-                    )
-
-        def finish_out0(t):
-            a = a_sb[t]
-            res = res_sb[t]
-            spare = ring.tile([P, D], BF16, name="spare", tag="staged_dz", bufs=3, align_bytes=64)
-            coef = ring.tile([P, 1], F32, name="coef", bufs=2)
-            h_t = h_raw[t // 2][:, t % 2, :]
-            g_t = g_raw[t // 2][:, t % 2, :]
-            nc.vector.scalar_tensor_tensor(
-                out=spare[:], in0=a[:], scalar=rr_cols[:, t : t + 1], in1=h_t, op0=ALU.mult, op1=ALU.mult, accum_out=coef[:],
-            )
-            if not G_C:
-                nc.vector.tensor_tensor(out=res[:], in0=a[:], in1=g_t, op=ALU.add)
-            for half in range(2):
-                nc.vector.scalar_tensor_tensor(
-                    out=res[:, halves[half]], in0=h_t[:, halves[half]], scalar=coef[:], in1=res[:, halves[half]],
-                    op0=ALU.mult, op1=ALU.add,
-                )
-            nc.sync.dma_start(out=out0_rows[:, t, :], in_=res[:])
-
-        def token_side(f):
-            il = ring.tile([P, 4 * N], BF16, name="il", tag="staged", bufs=4, align_bytes=64)
-            interleave(il[:], dz_bf[f][:], f in IL_ACT)
-            return il
-
-        def quantize_tok(f, il):
-            dz_tok[f] = operand(ring, "dzt", N, bufs=DZT_BUFS)
-            quantize(dz_tok[f], il[:], E5M2)
-
-        warm(WARM)
-        for j in range(4):
-            hn_part(j)
-        staged = turn(g_raw, "slot major", WARM_MID)
-        for g in range(2):
-            quantize(g_op[g], staged[g][:], E5M2)
-        hn_interleave()
-        quantize_wv(0, turn_weight("wv", 0, "row major", WARM_MID))
-        quantize(hn_op, hn_state["il"][:], E4M3)
-        nc.vector.tensor_scalar(out=r2_cols[:], in0=r_cols[:], scalar1=2.0, scalar2=None, op0=ALU.mult)
-        nc.vector.scalar_tensor_tensor(
-            out=rr_cols[:], in0=r_cols[:], scalar=-1.0 / D, in1=r_cols[:], op0=ALU.mult, op1=ALU.mult
-        )
-
-        last = CHUNKS - 1
-        staged_dz = {}
-
-        def both(f, t):
-            dk(f, t)
-            dz(f, t)
-
-        def feat(f, pair):
-            quantize_dz_feat(f, pair, staged_dz[f, pair])
-
-        for f in range(CHUNKS):
-            full = f < FULL
-            if f < last:
-                staged_wv = turn_weight("wv", f + 1, "row major", WARM_MID if f == 0 else 0)
-            dz_bf[f] = ring.tile([P, 4, N], BF16, name="dz_bf", bufs=DZ_BUFS)
-            both(f, 0)
-            if full:
-                both(f, 1)
-            weave(O1_A[f], [])
-            if f < last:
-                quantize_wv(f + 1, staged_wv)
-            staged_wk = turn_weight("wk", f, "slot major")
-            if full:
-                both(f, 2)
-                both(f, 3)
-            else:
-                both(f, 1)
-            weave(O1_B[f], [])
-            quantize_wk(f, staged_wk)
-            if full:
-                il = token_side(f)
+                hn_interleaved = interleave("hn_interleaved", hn_bf16, tag="out1", bufs=OUT1_BUFS)
+            staged_wk = turn_weight("wk", f, "e c", False)
+            for t in (1,) if late else (2, 3):
+                make_dz(f, t)
             if f > 0:
-                for pair in range(2 if f - 1 < FULL else 1):
-                    staged_dz[f - 1, pair] = turn_dz(f - 1, pair)
-                    feat(f - 1, pair)
-            if full:
-                quantize_tok(f, il)
+                out1_tiles(per_gap)
+            quantize_wk(f, staged_wk)
+            if not late:
+                staged_tok = interleave_dz(f)
+            if f > 0:
+                for pair in range(2):
+                    quantize_dz_feat(f - 1, pair, turn_dz(f - 1, pair))
+            if not late:
+                quantize_dz_tok(f, staged_tok)
+            if f == 0:
+                hn_mx = quantize(keep, "hn", hn_interleaved, E4M3)
 
-        def passes(t, chunks):
-            return [(t, half, f) for half in range(2) for f in chunks]
+        make_dz(LAST, 0)
+        make_dz(LAST, 1)
+        out1_tiles(OUT1_PER_LATE_GAP)
+        staged_wk = new_staged()
+        for pair in range(2):
+            turn_pair(loaded["wk", LAST, pair], pair, staged_wk, "e c")
+            issue_loads(("wk", LAST, pair))
+            make_dz(LAST - 1, 2 + pair)
+        out1_tiles(OUT1_PER_LATE_GAP)
+        quantize_wk(LAST, staged_wk)
+        for f in LATE_CHUNKS:
+            quantize_dz_feat(f, 0, turn_dz(f, 0))
+        make_dz(LAST, 2)
+        make_dz(LAST, 3)
+        staged_tok = interleave_dz(LAST - 1)
+        sums = dhn_with_out1(0)
+        quantize_dz_tok(LAST - 1, staged_tok)
+        rn = scale_dhn(0, sums)
+        staged_feat = [turn_dz(f, 1) for f in LATE_CHUNKS]
+        staged_tok = interleave_dz(LAST)
+        for f, staged in zip(LATE_CHUNKS, staged_feat):
+            quantize_dz_feat(f, 1, staged)
+        quantize_dz_tok(LAST, staged_tok)
 
-        every = list(range(CHUNKS))
-        lag = CHUNKS - FULL
-        staged_dz[last, 0] = turn_dz(last, 0)
-        for s in range(lag):
-            c = FULL + s
-            dk(c, 2)
-            dk(c, 3)
-            if s > 0:
-                staged_dz[c - 1, 1] = turn_dz(c - 1, 1)
-                dhn_read(s - 1)
-            dz(c, 2)
-            dz(c, 3)
-            if s == 0:
-                feat(last, 0)
-            else:
-                feat(c - 1, 1)
-            il = token_side(c)
-            if c == last:
-                staged_dz[last, 1] = turn_dz(last, 1)
-                feat(last, 1)
-            quantize_tok(c, il)
-            weave(O1_C[s], passes(s, every))
-            if s > 0:
-                finish_out0(s - 1)
-        for s in range(lag, 4):
-            dhn_read(s - 1)
-            weave(O1_C[s], passes(s, every))
-            finish_out0(s - 1)
-        dhn_read(3)
-        weave(len(o1_todo), [])
-        finish_out0(3)
+        for t in range(1, SLOTS):
+            sums = dhn_with_out1(t)
+            finish_out0(t - 1, rn)
+            rn = scale_dhn(t, sums)
+        out1_tiles(len(out1_todo))
+        finish_out0(SLOTS - 1, rn)

@@ -22,21 +22,19 @@ SLOTS = 4
 BANKS = 8
 ALIGN = 64
 
-LATE_CHUNKS = (LAST - 1, LAST)
-
 OUT1_PER_GAP = 3
-OUT1_PER_LATE_GAP = 2
-OUT1_PER_DHN = 6
+OUT1_IN_LAST_STEP = 2
+DHN_PASSES_PER_OUT1 = 2
 
 WARM_FIRST = 7
 
-WEIGHT_BUFS = 6
+WEIGHT_BUFS = 7
 Z_BUFS = 4
-STAGED_BUFS = 4
+STAGED_BUFS = 5
 HALF_STAGED_BUFS = 3
 OUT1_BUFS = 5
-WV_BUFS = 6
-DZ_BUFS = 3
+WV_BUFS = 4
+DZ_BUFS = 2
 DZ_TOK_BUFS = 5
 
 
@@ -85,11 +83,7 @@ def tile_block_pc_v_kernel(tc, h_attn, norm2_w, ffn_wk, ffn_wv, z, rstd, grad_ou
         for f in range(CHUNKS):
             if f < LAST:
                 stream.extend([("wv", f + 1, 0), ("wv", f + 1, 1)])
-            stream.extend([("z", f, 0), ("wk", f, 0)])
-            if f not in LATE_CHUNKS:
-                stream.append(("z", f, 1))
-            stream.append(("wk", f, 1))
-        stream.extend([("z", f, 1) for f in LATE_CHUNKS])
+            stream.extend([("z", f, 0), ("wk", f, 0), ("z", f, 1), ("wk", f, 1)])
         loaded, consumed, held_stores = {}, set(), []
         issued = {"weights": [], "z": []}
 
@@ -157,14 +151,13 @@ def tile_block_pc_v_kernel(tc, h_attn, norm2_w, ffn_wk, ffn_wv, z, rstd, grad_ou
                         nc.tensor.transpose(turned[:, e, u, :], every_second, identity[:])
                 copy_turned(staged[k_pass][:].bitcast(F32)[:, pair * N : (pair + 1) * N], turned, column_order)
 
-        def turn_weight(kind, index, column_order, keep_warm):
+        def turn_weight(kind, index, column_order, between):
             staged = new_staged()
-            for pair in range(2):
-                turn_pair(loaded[kind, index, pair], pair, staged, column_order)
-                if keep_warm:
-                    warm(1)
+            turn_pair(loaded[kind, index, 0], 0, staged, column_order)
+            other = between()
+            turn_pair(loaded[kind, index, 1], 1, staged, column_order)
             issue_loads((kind, index, 0), (kind, index, 1))
-            return staged
+            return staged, other
 
         def interleave(name, source, **tile_options):
             out = ring.tile([P, SLOTS * source.shape[2]], BF16, name=name, align_bytes=ALIGN, **tile_options)
@@ -259,7 +252,7 @@ def tile_block_pc_v_kernel(tc, h_attn, norm2_w, ffn_wk, ffn_wv, z, rstd, grad_ou
         out1_todo = [(f, n) for f in range(CHUNKS) for n in range(D // P)]
         out1_sb = {}
 
-        def out1_tile():
+        def out1_tile(copy):
             f, n = out1_todo[0]
             out1_todo.remove((f, n))
             half, row = divmod(n, 4)
@@ -267,7 +260,7 @@ def tile_block_pc_v_kernel(tc, h_attn, norm2_w, ffn_wk, ffn_wv, z, rstd, grad_ou
                 out1_sb[f, half] = ring.tile([P, 4, N], F32, name="out1", tag="out1", bufs=OUT1_BUFS, align_bytes=ALIGN)
             acc = next_bank([P, N])
             mx_pass(acc, hn_mx, n * P, dz_tok_mx[f], True, True)
-            nc.scalar.copy(
+            copy(
                 out=out1_sb[f, half][:, row, :].rearrange("p (w u e) -> p w u e", u=2, e=2),
                 in_=acc[:].rearrange("p (u w e) -> p w u e", u=2, e=2),
             )
@@ -278,14 +271,14 @@ def tile_block_pc_v_kernel(tc, h_attn, norm2_w, ffn_wk, ffn_wv, z, rstd, grad_ou
 
         def out1_tiles(count):
             for repeat in range(count):
-                out1_tile()
+                out1_tile(nc.scalar.copy)
 
         def dhn_with_out1(t):
             sums = []
             for half in range(2):
                 for f in range(CHUNKS):
-                    if f % (2 * CHUNKS // OUT1_PER_DHN) == 0:
-                        out1_tile()
+                    if f % DHN_PASSES_PER_OUT1 == 0:
+                        out1_tiles(1)
                     if f == 0:
                         index = rotation[0]
                         sums.append((index, next_bank([P, N])))
@@ -351,61 +344,59 @@ def tile_block_pc_v_kernel(tc, h_attn, norm2_w, ffn_wk, ffn_wv, z, rstd, grad_ou
 
         make_hn(0)
         make_hn(1)
-        quantize_wv(0, turn_weight("wv", 0, "c e", True))
+        staged_wv, unused = turn_weight("wv", 0, "c e", lambda: warm(1))
+        warm(1)
+        quantize_wv(0, staged_wv)
         make_hn(2)
         make_hn(3)
 
-        for f in range(LAST):
-            late = f in LATE_CHUNKS
-            per_gap = OUT1_PER_LATE_GAP if late else OUT1_PER_GAP
-            staged_wv = turn_weight("wv", f + 1, "c e", f == 0)
+        staged_wv, unused = turn_weight("wv", 1, "c e", lambda: warm(1))
+        warm(1)
+        make_dz(0, 0)
+        make_dz(0, 1)
+        quantize_wv(1, staged_wv)
+        hn_interleaved = interleave("hn_interleaved", hn_bf16, tag="out1", bufs=OUT1_BUFS)
+        staged_wk, unused = turn_weight("wk", 0, "e c", lambda: make_dz(0, 2))
+        make_dz(0, 3)
+        quantize_wk(0, staged_wk)
+        staged_tok = interleave_dz(0)
+        hn_mx = quantize(keep, "hn", hn_interleaved, E4M3)
+        quantize_dz_tok(0, staged_tok)
+
+        for f in range(1, LAST):
+            staged_wv, staged_feat = turn_weight("wv", f + 1, "c e", lambda: turn_dz(f - 1, 0))
             make_dz(f, 0)
-            if not late:
-                make_dz(f, 1)
+            make_dz(f, 1)
             if f > 1:
-                out1_tiles(per_gap)
+                out1_tile(nc.vector.tensor_copy)
+                out1_tiles(OUT1_PER_GAP - 1)
             quantize_wv(f + 1, staged_wv)
-            if f == 0:
-                hn_interleaved = interleave("hn_interleaved", hn_bf16, tag="out1", bufs=OUT1_BUFS)
-            staged_wk = turn_weight("wk", f, "e c", False)
-            for t in (1,) if late else (2, 3):
-                make_dz(f, t)
-            if f > 0:
-                out1_tiles(per_gap)
+            quantize_dz_feat(f - 1, 0, staged_feat)
+            staged_wk, staged_feat = turn_weight("wk", f, "e c", lambda: turn_dz(f - 1, 1))
+            make_dz(f, 2)
+            make_dz(f, 3)
+            out1_tiles(OUT1_PER_GAP)
             quantize_wk(f, staged_wk)
-            if not late:
-                staged_tok = interleave_dz(f)
-            if f > 0:
-                for pair in range(2):
-                    quantize_dz_feat(f - 1, pair, turn_dz(f - 1, pair))
-            if not late:
-                quantize_dz_tok(f, staged_tok)
-            if f == 0:
-                hn_mx = quantize(keep, "hn", hn_interleaved, E4M3)
+            staged_tok = interleave_dz(f)
+            quantize_dz_feat(f - 1, 1, staged_feat)
+            quantize_dz_tok(f, staged_tok)
 
         make_dz(LAST, 0)
         make_dz(LAST, 1)
-        out1_tiles(OUT1_PER_LATE_GAP)
+        out1_tiles(OUT1_IN_LAST_STEP)
         staged_wk = new_staged()
-        for pair in range(2):
-            turn_pair(loaded["wk", LAST, pair], pair, staged_wk, "e c")
-            issue_loads(("wk", LAST, pair))
-            make_dz(LAST - 1, 2 + pair)
-        out1_tiles(OUT1_PER_LATE_GAP)
-        quantize_wk(LAST, staged_wk)
-        for f in LATE_CHUNKS:
-            quantize_dz_feat(f, 0, turn_dz(f, 0))
+        turn_pair(loaded["wk", LAST, 0], 0, staged_wk, "e c")
         make_dz(LAST, 2)
         make_dz(LAST, 3)
-        staged_tok = interleave_dz(LAST - 1)
-        sums = dhn_with_out1(0)
-        quantize_dz_tok(LAST - 1, staged_tok)
-        rn = scale_dhn(0, sums)
-        staged_feat = [turn_dz(f, 1) for f in LATE_CHUNKS]
+        turn_pair(loaded["wk", LAST, 1], 1, staged_wk, "e c")
+        quantize_wk(LAST, staged_wk)
+        for f in (LAST - 1, LAST):
+            quantize_dz_feat(f, 0, turn_dz(f, 0))
         staged_tok = interleave_dz(LAST)
-        for f, staged in zip(LATE_CHUNKS, staged_feat):
-            quantize_dz_feat(f, 1, staged)
+        for f in (LAST - 1, LAST):
+            quantize_dz_feat(f, 1, turn_dz(f, 1))
         quantize_dz_tok(LAST, staged_tok)
+        rn = scale_dhn(0, dhn_with_out1(0))
 
         for t in range(1, SLOTS):
             sums = dhn_with_out1(t)

@@ -26,8 +26,6 @@ OUT1_PER_GAP = 3
 OUT1_IN_LAST_STEP = 2
 DHN_PASSES_PER_OUT1 = 2
 
-WARM_FIRST = 7
-
 WEIGHT_BUFS = 7
 Z_BUFS = 4
 STAGED_BUFS = 5
@@ -174,16 +172,6 @@ def tile_block_pc_v_kernel(tc, h_attn, norm2_w, ffn_wk, ffn_wv, z, rstd, grad_ou
         g_pairs = [load_pair(keep, "g%d" % pair, g_rows, pair) for pair in range(2)]
         issue_loads()
 
-        zeros = keep.tile([P, N], BF16, name="zeros")
-        nc.vector.memset(zeros[:], 0.0)
-
-        def warm(count):
-            unread = next_bank([P, N])
-            for repeat in range(count):
-                nc.tensor.matmul(unread[:], lhsT=zeros[:, 0:P], rhs=zeros[:], start=True, stop=True)
-
-        warm(WARM_FIRST)
-
         w_turned = next_bank([P, 4, P])
         w_words = w_columns[:].bitcast(F32)
         for j in range(4):
@@ -324,7 +312,6 @@ def tile_block_pc_v_kernel(tc, h_attn, norm2_w, ffn_wk, ffn_wv, z, rstd, grad_ou
         staged_g = new_staged()
         for pair in range(2):
             turn_pair(g_pairs[pair], pair, staged_g, "e c")
-            warm(1)
         g_mx = [quantize(keep, "g%d" % k_pass, staged_g[k_pass], E5M2) for k_pass in range(2)]
 
         rstd_columns = loaded["rstd", 0, 0]
@@ -344,14 +331,12 @@ def tile_block_pc_v_kernel(tc, h_attn, norm2_w, ffn_wk, ffn_wv, z, rstd, grad_ou
 
         make_hn(0)
         make_hn(1)
-        staged_wv, unused = turn_weight("wv", 0, "c e", lambda: warm(1))
-        warm(1)
+        staged_wv, unused = turn_weight("wv", 0, "c e", lambda: None)
         quantize_wv(0, staged_wv)
         make_hn(2)
         make_hn(3)
 
-        staged_wv, unused = turn_weight("wv", 1, "c e", lambda: warm(1))
-        warm(1)
+        staged_wv, unused = turn_weight("wv", 1, "c e", lambda: None)
         make_dz(0, 0)
         make_dz(0, 1)
         quantize_wv(1, staged_wv)

from contextlib import ExitStack

import concourse.mybir as mybir
from concourse.masks import make_identity

T, D, FF = 512, 1024, 3072
FLOPS = 3 * 2 * T * D * FF

F32 = mybir.dt.float32
BF16 = mybir.dt.bfloat16
U32 = mybir.dt.uint32
U8 = mybir.dt.uint8
E4M3 = mybir.dt.float8_e4m3fn_x4
E5M2 = mybir.dt.float8_e5m2_x4
ALU = mybir.AluOpType

P = 128
N = 512
CHUNKS = FF // N
LAST = CHUNKS - 1
SLOTS = 4
BANKS = 8
ALIGN = 64

OUT1_PER_GAP = 3
OUT1_IN_LAST_STEP = 2
DHN_PASSES_PER_OUT1 = 2

WEIGHT_BUFS = 7
Z_BUFS = 4
STAGED_BUFS = 5
HALF_STAGED_BUFS = 3
OUT1_BUFS = 5
WV_BUFS = 4
DZ_BUFS = 2
DZ_TOK_BUFS = 5


def tile_block_pc_v_kernel(tc, h_attn, norm2_w, ffn_wk, ffn_wv, z, rstd, grad_out, out_0, out_1):
    nc = tc.nc
    h_rows = h_attn.rearrange("b (p t) d -> p (b t) d", t=SLOTS)
    g_rows = grad_out.rearrange("b (p t) d -> p (b t) d", t=SLOTS)
    z_rows = z.rearrange("b (p t) f -> p (b t) f", t=SLOTS)
    out0_rows = out_0.rearrange("b (p t) d -> p (b t) d", t=SLOTS)
    d_halves = [slice(0, N), slice(N, D)]

    with ExitStack() as ctx:
        keep = ctx.enter_context(tc.tile_pool(name="keep", bufs=1))
        ring = ctx.enter_context(tc.tile_pool(name="ring", bufs=2))
        psum = ctx.enter_context(tc.psum_pool(name="psum", bufs=1))
        ctx.enter_context(tc.manual_schedule())

        rotation = list(range(BANKS))

        def next_bank(shape):
            index = rotation[0]
            rotation.remove(index)
            rotation.append(index)
            return psum.tile(shape, F32, name="bank%d" % index, tag="bank%d" % index)

        def quantize(pool, name, staged, fmt, **ring_depth):
            width = staged.shape[1] // 4
            codes = pool.tile([P, width], U32, name=name + "_codes", align_bytes=ALIGN, **ring_depth)
            scales = pool.tile([P, width], U8, name=name + "_scales", align_bytes=ALIGN, **ring_depth)
            nc.vector.quantize_mx(out=codes[:].bitcast(fmt), scales=scales[:], in_=staged[:])
            return codes, scales, fmt

        def mx_pass(acc, stationary, first_column, moving, start, stop):
            columns = slice(first_column, first_column + P)
            nc.tensor.matmul_mx(
                out=acc[:],
                lhsT=stationary[0][:, columns].bitcast(stationary[2]),
                lhsT_scale=stationary[1][:, columns],
                rhs=moving[0][:].bitcast(moving[2]),
                rhs_scale=moving[1][:],
                start=start,
                stop=stop,
            )

        stream = [("rstd", 0, 0), ("h", 0, 0), ("wv", 0, 0), ("wv", 0, 1), ("h", 0, 1)]
        for f in range(CHUNKS):
            if f < LAST:
                stream.extend([("wv", f + 1, 0), ("wv", f + 1, 1)])
            stream.extend([("z", f, 0), ("wk", f, 0), ("z", f, 1), ("wk", f, 1)])
        loaded, consumed, held_stores = {}, set(), []
        issued = {"weights": [], "z": []}

        def load_pair(pool, name, rows, pair, **ring_depth):
            tile = pool.tile([P, 2, rows.shape[2]], rows.dtype, name=name, **ring_depth)
            nc.sync.dma_start(out=tile[:], in_=rows[:, 2 * pair : 2 * pair + 2, :])
            return tile

        def load(kind, index, pair):
            if kind == "rstd":
                tile = keep.tile([P, SLOTS], F32, name="rstd")
                nc.sync.dma_start(out=tile[:], in_=rstd.rearrange("b (p t) o -> p (b t o)", t=SLOTS))
                return tile
            if kind == "h":
                return load_pair(keep, "h%d" % pair, h_rows, pair)
            if kind == "z":
                return load_pair(ring, "z", z_rows[:, :, index * N : (index + 1) * N], pair, bufs=Z_BUFS)
            if kind == "wv":
                rows = ffn_wv[index * N : (index + 1) * N, :].rearrange("(p r) k -> p r k", r=4)
            else:
                chunk_pair, half = divmod(index, 2)
                rows = ffn_wk[d_halves[half], chunk_pair * 2 * N : (chunk_pair + 1) * 2 * N]
                rows = rows.rearrange("(r p) k -> p r k", p=P)
            return load_pair(ring, "weight", rows, pair, bufs=WEIGHT_BUFS)

        def issue_stores(keep_back):
            while len(held_stores) > keep_back:
                dst, tile = held_stores[0]
                nc.sync.dma_start(out=dst, in_=tile[:])
                held_stores[:] = held_stores[1:]

        def issue_loads(*just_read):
            for item in just_read:
                consumed.add(item)
            while stream:
                item = stream[0]
                if item[0] in ("wv", "wk", "z"):
                    earlier, depth = (issued["z"], Z_BUFS) if item[0] == "z" else (issued["weights"], WEIGHT_BUFS)
                    if len(earlier) >= depth and earlier[len(earlier) - depth] not in consumed:
                        return
                    earlier.append(item)
                loaded[item] = load(*item)
                stream.remove(item)
            issue_stores(0)

        def copy_turned(dst_words, turned, column_order):
            nc.scalar.copy(
                out=dst_words.rearrange("p (%s u) -> p %s u" % (column_order, column_order), e=2, u=2),
                in_=turned[:].rearrange("p e u c -> p %s u" % column_order),
            )

        def new_staged():
            return [
                ring.tile([P, 4 * N], BF16, name="staged", tag="staged", bufs=STAGED_BUFS, align_bytes=ALIGN)
                for k_pass in range(2)
            ]

        def turn_pair(source, pair, staged, column_order):
            words = source[:].bitcast(F32)
            for k_pass in range(2):
                turned = next_bank([P, 2, 2, P])
                for e in range(2):
                    for u in range(2):
                        every_second = words[:, e, 256 * k_pass + u : 256 * (k_pass + 1) : 2]
                        nc.tensor.transpose(turned[:, e, u, :], every_second, identity[:])
                copy_turned(staged[k_pass][:].bitcast(F32)[:, pair * N : (pair + 1) * N], turned, column_order)

        def turn_weight(kind, index, column_order, between):
            staged = new_staged()
            turn_pair(loaded[kind, index, 0], 0, staged, column_order)
            other = between()
            turn_pair(loaded[kind, index, 1], 1, staged, column_order)
            issue_loads((kind, index, 0), (kind, index, 1))
            return staged, other

        def interleave(name, source, **tile_options):
            out = ring.tile([P, SLOTS * source.shape[2]], BF16, name=name, align_bytes=ALIGN, **tile_options)
            nc.vector.tensor_copy(
                out=out[:].rearrange("p (c i t) -> p c t i", i=4, t=SLOTS),
                in_=source[:].rearrange("p t (c i) -> p c t i", i=4),
            )
            return out

        identity = keep.tile([P, P], F32, name="identity")
        make_identity(nc, identity[:])
        w_columns = keep.tile([P, 8], BF16, name="w_columns")
        nc.sync.dma_start(out=w_columns[:], in_=norm2_w.rearrange("(p j) -> p j", j=8))
        g_pairs = [load_pair(keep, "g%d" % pair, g_rows, pair) for pair in range(2)]
        issue_loads()

        w_turned = next_bank([P, 4, P])
        w_words = w_columns[:].bitcast(F32)
        for j in range(4):
            nc.tensor.transpose(w_turned[:, j, :], w_words[:, j : j + 1].to_broadcast([P, P]), identity[:])
        w_row = keep.tile([P, D], BF16, name="w_row")
        nc.scalar.copy(
            out=w_row[:].bitcast(F32).rearrange("p (c j) -> p c j", j=4),
            in_=w_turned[:].rearrange("p j c -> p c j"),
        )

        def h_slot(t):
            return loaded["h", 0, t // 2][:, t % 2, :]

        wv_mx, wk_mx, dz_bf16, dz_tok_mx, dz_feat_mx = {}, {}, {}, {}, {}

        def quantize_wv(f, staged):
            wv_mx[f] = [quantize(ring, "wv", staged[k_pass], E4M3, bufs=WV_BUFS) for k_pass in range(2)]

        def quantize_wk(index, staged):
            chunk_pair, half = divmod(index, 2)
            for k_pass in range(2):
                f = 2 * chunk_pair + k_pass
                wk_mx[f, half] = quantize(keep, "wk%d_%d" % (f, half), staged[k_pass], E4M3)

        def make_dz(f, t):
            if t == 0:
                dz_bf16[f] = ring.tile([P, SLOTS, N], BF16, name="dz_bf16", bufs=DZ_BUFS)
            dk = next_bank([P, N])
            for k_pass in range(2):
                mx_pass(dk, g_mx[k_pass], t * P, wv_mx[f][k_pass], k_pass == 0, k_pass == 1)
            z_view = loaded["z", f, t // 2][:, t % 2, :].rearrange("p (w u e) -> p u w e", u=2, e=2)
            for u in range(2):
                columns = slice(u * 256, (u + 1) * 256)
                nc.vector.scalar_tensor_tensor(
                    out=dz_bf16[f][:, t, columns].rearrange("p (w e) -> p w e", e=2),
                    in0=z_view[:, u, :, :],
                    scalar=0.0,
                    in1=dk[:, columns].rearrange("p (w e) -> p w e", e=2),
                    op0=ALU.max,
                    op1=ALU.mult,
                )
            if t % 2:
                issue_loads(("z", f, t // 2))

        def turn_dz(f, pair):
            staged = ring.tile(
                [P, 2 * N], BF16, name="staged_dz", tag="half_staged", bufs=HALF_STAGED_BUFS, align_bytes=ALIGN
            )
            words = dz_bf16[f][:].bitcast(F32)
            turned = next_bank([P, 2, 2, P])
            for e in range(2):
                for u in range(2):
                    nc.tensor.transpose(turned[:, e, u, :], words[:, 2 * pair + e, u * P : (u + 1) * P], identity[:])
            copy_turned(staged[:].bitcast(F32), turned, "e c")
            return staged

        def quantize_dz_feat(f, pair, staged):
            dz_feat_mx[f, pair] = quantize(keep, "dz_feat%d_%d" % (f, pair), staged, E5M2)

        def interleave_dz(f):
            return interleave("dz_interleaved", dz_bf16[f], tag="staged", bufs=STAGED_BUFS)

        def quantize_dz_tok(f, staged):
            dz_tok_mx[f] = quantize(ring, "dz_tok", staged, E5M2, bufs=DZ_TOK_BUFS)

        out1_todo = [(f, n) for f in range(CHUNKS) for n in range(D // P)]
        out1_sb = {}

        def out1_tile(copy):
            f, n = out1_todo[0]
            out1_todo.remove((f, n))
            half, row = divmod(n, 4)
            if row == 0:
                out1_sb[f, half] = ring.tile([P, 4, N], F32, name="out1", tag="out1", bufs=OUT1_BUFS, align_bytes=ALIGN)
            acc = next_bank([P, N])
            mx_pass(acc, hn_mx, n * P, dz_tok_mx[f], True, True)
            copy(
                out=out1_sb[f, half][:, row, :].rearrange("p (w u e) -> p w u e", u=2, e=2),
                in_=acc[:].rearrange("p (u w e) -> p w u e", u=2, e=2),
            )
            if row == 3:
                dst = out_1[d_halves[half], f * N : (f + 1) * N].rearrange("(n p) c -> p n c", p=P)
                held_stores.append((dst, out1_sb[f, half]))
                issue_stores(OUT1_BUFS - 1 if stream else 0)

        def out1_tiles(count):
            for repeat in range(count):
                out1_tile(nc.scalar.copy)

        def dhn_with_out1(t):
            sums = []
            for half in range(2):
                for f in range(CHUNKS):
                    if f % DHN_PASSES_PER_OUT1 == 0:
                        out1_tiles(1)
                    if f == 0:
                        index = rotation[0]
                        sums.append((index, next_bank([P, N])))
                        rotation.remove(index)
                    mx_pass(sums[half][1], dz_feat_mx[f, t // 2], (t % 2) * P, wk_mx[f, half], f == 0, f == LAST)
            return sums

        def scale_dhn(t, sums):
            rn = ring.tile([P, D], F32, name="rn", bufs=2)
            for half in range(2):
                index, acc = sums[half]
                nc.vector.scalar_tensor_tensor(
                    out=rn[:, d_halves[half]], in0=acc[:], scalar=two_rstd[:, t : t + 1], in1=w_row[:, d_halves[half]],
                    op0=ALU.mult, op1=ALU.mult,
                )
                rotation.append(index)
            return rn

        def finish_out0(t, rn):
            result = ring.tile([P, D], F32, name="result", bufs=2)
            products = ring.tile(
                [P, D], BF16, name="products", tag="half_staged", bufs=HALF_STAGED_BUFS, align_bytes=ALIGN
            )
            coef = ring.tile([P, 1], F32, name="coef", bufs=2)
            g_slot = g_pairs[t // 2][:, t % 2, :]
            low, high = d_halves
            nc.vector.tensor_tensor(out=result[:, low], in0=rn[:, low], in1=g_slot[:, low], op=ALU.add)
            nc.vector.scalar_tensor_tensor(
                out=products[:], in0=rn[:], scalar=mean_factor[:, t : t + 1], in1=h_slot(t),
                op0=ALU.mult, op1=ALU.mult, accum_out=coef[:],
            )
            nc.vector.tensor_tensor(out=result[:, high], in0=rn[:, high], in1=g_slot[:, high], op=ALU.add)
            for columns in d_halves:
                nc.vector.scalar_tensor_tensor(
                    out=result[:, columns], in0=h_slot(t)[:, columns], scalar=coef[:], in1=result[:, columns],
                    op0=ALU.mult, op1=ALU.add,
                )
                if t == SLOTS - 1:
                    nc.sync.dma_start(out=out0_rows[:, t, columns], in_=result[:, columns])
            if t < SLOTS - 1:
                nc.sync.dma_start(out=out0_rows[:, t, :], in_=result[:])

        staged_g = new_staged()
        for pair in range(2):
            turn_pair(g_pairs[pair], pair, staged_g, "e c")
        g_mx = [quantize(keep, "g%d" % k_pass, staged_g[k_pass], E5M2) for k_pass in range(2)]

        rstd_columns = loaded["rstd", 0, 0]
        two_rstd = keep.tile([P, SLOTS], F32, name="two_rstd")
        nc.vector.tensor_scalar(out=two_rstd[:], in0=rstd_columns[:], scalar1=2.0, scalar2=None, op0=ALU.mult)
        mean_factor = keep.tile([P, SLOTS], F32, name="mean_factor")
        nc.vector.scalar_tensor_tensor(
            out=mean_factor[:], in0=rstd_columns[:], scalar=-1.0 / D, in1=rstd_columns[:], op0=ALU.mult, op1=ALU.mult
        )
        hn_bf16 = ring.tile([P, SLOTS, D], BF16, name="hn_bf16", tag="out1", bufs=OUT1_BUFS, align_bytes=ALIGN)

        def make_hn(t):
            nc.vector.scalar_tensor_tensor(
                out=hn_bf16[:, t, :], in0=h_slot(t), scalar=two_rstd[:, t : t + 1], in1=w_row[:],
                op0=ALU.mult, op1=ALU.mult,
            )

        make_hn(0)
        make_hn(1)
        staged_wv, unused = turn_weight("wv", 0, "c e", lambda: None)
        quantize_wv(0, staged_wv)
        make_hn(2)
        make_hn(3)

        staged_wv, unused = turn_weight("wv", 1, "c e", lambda: None)
        make_dz(0, 0)
        make_dz(0, 1)
        quantize_wv(1, staged_wv)
        hn_interleaved = interleave("hn_interleaved", hn_bf16, tag="out1", bufs=OUT1_BUFS)
        staged_wk, unused = turn_weight("wk", 0, "e c", lambda: make_dz(0, 2))
        make_dz(0, 3)
        quantize_wk(0, staged_wk)
        staged_tok = interleave_dz(0)
        hn_mx = quantize(keep, "hn", hn_interleaved, E4M3)
        quantize_dz_tok(0, staged_tok)

        for f in range(1, LAST):
            staged_wv, staged_feat = turn_weight("wv", f + 1, "c e", lambda: turn_dz(f - 1, 0))
            make_dz(f, 0)
            make_dz(f, 1)
            if f > 1:
                out1_tile(nc.vector.tensor_copy)
                out1_tiles(OUT1_PER_GAP - 1)
            quantize_wv(f + 1, staged_wv)
            quantize_dz_feat(f - 1, 0, staged_feat)
            staged_wk, staged_feat = turn_weight("wk", f, "e c", lambda: turn_dz(f - 1, 1))
            make_dz(f, 2)
            make_dz(f, 3)
            out1_tiles(OUT1_PER_GAP)
            quantize_wk(f, staged_wk)
            staged_tok = interleave_dz(f)
            quantize_dz_feat(f - 1, 1, staged_feat)
            quantize_dz_tok(f, staged_tok)

        make_dz(LAST, 0)
        make_dz(LAST, 1)
        out1_tiles(OUT1_IN_LAST_STEP)
        staged_wk = new_staged()
        turn_pair(loaded["wk", LAST, 0], 0, staged_wk, "e c")
        make_dz(LAST, 2)
        make_dz(LAST, 3)
        turn_pair(loaded["wk", LAST, 1], 1, staged_wk, "e c")
        quantize_wk(LAST, staged_wk)
        for f in (LAST - 1, LAST):
            quantize_dz_feat(f, 0, turn_dz(f, 0))
        staged_tok = interleave_dz(LAST)
        for f in (LAST - 1, LAST):
            quantize_dz_feat(f, 1, turn_dz(f, 1))
        quantize_dz_tok(LAST, staged_tok)
        rn = scale_dhn(0, dhn_with_out1(0))

        for t in range(1, SLOTS):
            sums = dhn_with_out1(t)
            finish_out0(t - 1, rn)
            rn = scale_dhn(t, sums)
        out1_tiles(len(out1_todo))
        finish_out0(SLOTS - 1, rn)
